import numpy as np
import ml_dtypes


def mxq(x, axis, fmt="e4m3"):
    dtype, down = {"e4m3": (ml_dtypes.float8_e4m3fn, 7), "e5m2": (ml_dtypes.float8_e5m2, 14)}[fmt]
    v = np.moveaxis(np.asarray(x, np.float32).astype(ml_dtypes.bfloat16).astype(np.float64), axis, -1)
    blocks = v.reshape(v.shape[:-1] + (-1, 32))
    amax = np.abs(blocks).max(-1, keepdims=True)
    byte = np.maximum(np.where(amax > 0, np.frexp(amax)[1] - 1 + 127, 0) - down, 1)
    scale = np.exp2(byte - 127.0)
    codes = (blocks / scale).astype(np.float32).astype(dtype).astype(np.float64)
    return np.moveaxis((codes * scale).reshape(v.shape), -1, axis)


WIDE = False


def mx_kscale(k):
    if not WIDE:
        return np.ones(k)
    levels = np.array([10, -10, 5, -5, 0])
    a = np.random.permutation(np.resize(levels, k // 512 * 4)).reshape(k // 512, 4)
    idx = np.arange(k)
    return np.exp2(a[idx // 512, idx % 128 // 32])


BF16 = ml_dtypes.bfloat16


def bf(x):
    return np.asarray(x, np.float32).astype(BF16)


def f64(x):
    return np.asarray(x).astype(np.float64)


B, IN, OUT, R, Q, ORD = 2048, 1024, 1024, 8, 256, 3
K = R ** ORD


def setup_inputs():
    s = mx_kscale(K)[np.arange(R) * (K // R + R)]
    z = np.random.standard_normal((ORD, R, B))
    z[ORD - 1] *= s[:, None]
    g = np.random.standard_normal((Q, K)) / np.sqrt(K) / np.repeat(s, K // R)
    return {"z": bf(z), "G2": bf(g)}


def reference(z, G2):
    Z = f64(z)
    kron = Z[0]
    for j in range(1, ORD):
        kron = kron[None] * Z[j].reshape((R,) + (1,) * j + (B,))
    kron = kron.reshape((-1, B))
    return mxq(f64(G2), 1, "e4m3") @ mxq(kron, 0, "e4m3")

@@ -1,0 +1,156 @@
+from contextlib import ExitStack
+
+import concourse.mybir as mybir
+from concourse.masks import make_identity
+
+F32 = mybir.dt.float32
+BF16 = mybir.dt.bfloat16
+U32 = mybir.dt.uint32
+U8 = mybir.dt.uint8
+FP8X4 = mybir.dt.float8_e4m3fn_x4
+MULT = mybir.AluOpType.mult
+
+P = 128
+ORD = 3
+R = 8
+K = R**ORD
+PACK = 4
+PAIRS = 2
+N = 2048
+M = 256
+N_TILES = N // P
+M_TILES = M // P
+CHUNK_TILES = 4
+CHUNK = CHUNK_TILES * P
+CHUNKS = N_TILES // CHUNK_TILES
+BANK_TILES = 2
+
+FLOPS = 2 * M * K * N
+
+
+def tile_fast_tucker_taylor_pa_s_kernel(tc, z, G2, out):
+    nc = tc.nc
+    with ExitStack() as ctx:
+        keep = ctx.enter_context(tc.tile_pool(name="keep", bufs=1))
+        work = ctx.enter_context(tc.tile_pool(name="work", bufs=2))
+        psum_once = ctx.enter_context(tc.psum_pool(name="psum_once", bufs=1))
+        psum_turn = ctx.enter_context(tc.psum_pool(name="psum_turn", bufs=3))
+        psum_acc = ctx.enter_context(tc.psum_pool(name="psum_acc", bufs=3))
+
+        z_rows = keep.tile([P, ORD, P], BF16)
+        nc.sync.dma_start(out=z_rows[:], in_=z.rearrange("i a (j s) -> (a j) i s", s=P))
+        g_rows = keep.tile([P, M_TILES, K], BF16)
+        nc.sync.dma_start(out=g_rows[:], in_=G2.rearrange("(h m) k -> m h k", m=P))
+
+        ident_bf16 = keep.tile([P, P], BF16)
+        make_identity(nc, ident_bf16[:])
+        ident_f32 = keep.tile([P, P], F32)
+        make_identity(nc, ident_f32[:])
+
+        zT_ps = psum_once.tile([P, ORD, P], BF16)
+        for i in range(ORD):
+            nc.tensor.transpose(out=zT_ps[:, i, :], in_=z_rows[:, i, :], identity=ident_bf16[:])
+        zT = keep.tile([P, ORD, N_TILES, R], F32)
+        nc.vector.tensor_copy(
+            out=zT[:], in_=zT_ps[:].rearrange("s i (a j) -> s i j a", j=N_TILES)
+        )
+
+        g_words = g_rows[:].bitcast(F32).rearrange("m h (q u) -> m h q u", u=PAIRS)
+        gT_ps = psum_once.tile([P, M_TILES, PAIRS, P], F32)
+        for h in range(M_TILES):
+            for u in range(PAIRS):
+                nc.tensor.transpose(
+                    out=gT_ps[:, h, u, :], in_=g_words[:, h, :, u], identity=ident_f32[:]
+                )
+        g_grouped = keep.tile([P, M * PACK], BF16, align_bytes=64)
+        nc.scalar.copy(
+            out=g_grouped[:].bitcast(F32).rearrange("q (h m u) -> q h m u", h=M_TILES, u=PAIRS),
+            in_=gT_ps[:].rearrange("q h u m -> q h m u"),
+        )
+        g_codes = keep.tile([P, M], U32, align_bytes=64)
+        g_scales = keep.tile([P, M], U8, align_bytes=64)
+
+        kronT_of = {}
+        grouped_of = {}
+
+        def multiply(g):
+            tiles = slice(g * CHUNK_TILES, (g + 1) * CHUNK_TILES)
+            pair = work.tile([P, CHUNK_TILES, R, R], F32)
+            nc.vector.tensor_tensor(
+                out=pair[:],
+                in0=zT[:, 0, tiles, :].unsqueeze(2).to_broadcast([P, CHUNK_TILES, R, R]),
+                in1=zT[:, 1, tiles, :].unsqueeze(3).to_broadcast([P, CHUNK_TILES, R, R]),
+                op=MULT,
+            )
+            kronT = work.tile([P, CHUNK_TILES, R, R * R], BF16)
+            nc.vector.tensor_tensor(
+                out=kronT[:],
+                in0=pair[:]
+                .rearrange("s j b a -> s j (b a)")
+                .unsqueeze(2)
+                .to_broadcast([P, CHUNK_TILES, R, R * R]),
+                in1=zT[:, 2, tiles, :].unsqueeze(3).to_broadcast([P, CHUNK_TILES, R, R * R]),
+                op=MULT,
+            )
+            kronT_of[g] = kronT
+
+        def turn(g):
+            words = (
+                kronT_of[g][:]
+                .rearrange("s j c x -> s j (c x)")
+                .bitcast(F32)
+                .rearrange("s j (q u) -> s j q u", u=PAIRS)
+            )
+            grouped = work.tile([P, CHUNK * PACK], BF16, align_bytes=64)
+            grouped_words = grouped[:].bitcast(F32).rearrange(
+                "q (j s u) -> q j s u", j=CHUNK_TILES, u=PAIRS
+            )
+            for first in range(0, CHUNK_TILES, BANK_TILES):
+                turned = psum_turn.tile([P, BANK_TILES, PAIRS, P], F32)
+                for t in range(BANK_TILES):
+                    for u in range(PAIRS):
+                        nc.tensor.transpose(
+                            out=turned[:, t, u, :],
+                            in_=words[:, first + t, :, u],
+                            identity=ident_f32[:],
+                        )
+                nc.scalar.copy(
+                    out=grouped_words[:, first : first + BANK_TILES, :, :],
+                    in_=turned[:].rearrange("q t u s -> q t s u"),
+                )
+            grouped_of[g] = grouped
+
+        def contract(g):
+            k_codes = work.tile([P, CHUNK], U32, align_bytes=64)
+            k_scales = work.tile([P, CHUNK], U8, align_bytes=64)
+            nc.vector.quantize_mx(
+                out=k_codes[:].bitcast(FP8X4), scales=k_scales[:], in_=grouped_of[g][:]
+            )
+            for h in range(M_TILES):
+                rows = slice(h * P, (h + 1) * P)
+                acc = psum_acc.tile([P, CHUNK], F32)
+                nc.tensor.matmul_mx(
+                    out=acc[:],
+                    lhsT=g_codes[:, rows].bitcast(FP8X4),
+                    lhsT_scale=g_scales[:, rows],
+                    rhs=k_codes[:].bitcast(FP8X4),
+                    rhs_scale=k_scales[:],
+                    start=True,
+                    stop=True,
+                )
+                result = work.tile([P, CHUNK], F32, bufs=4)
+                nc.scalar.copy(out=result[:], in_=acc[:])
+                nc.sync.dma_start(out=out[rows, g * CHUNK : (g + 1) * CHUNK], in_=result[:])
+
+        multiply(0)
+        nc.vector.quantize_mx(
+            out=g_codes[:].bitcast(FP8X4), scales=g_scales[:], in_=g_grouped[:]
+        )
+        turn(0)
+        multiply(1)
+        for g in range(CHUNKS):
+            if g + 1 < CHUNKS:
+                turn(g + 1)
+            contract(g)
+            if g + 2 < CHUNKS:
+                multiply(g + 2)

@@ -20,10 +20,11 @@ N = 2048
 M = 256
 N_TILES = N // P
 M_TILES = M // P
-CHUNK_TILES = 4
-CHUNK = CHUNK_TILES * P
-CHUNKS = N_TILES // CHUNK_TILES
-BANK_TILES = 2
+UNIT_TILES = 2
+UNIT = UNIT_TILES * P
+UNITS = N_TILES // UNIT_TILES
+C_POOL = 3
+C_VECTOR = R - C_POOL
 
 FLOPS = 2 * M * K * N
 
@@ -32,7 +33,7 @@ def tile_fast_tucker_taylor_pa_s_kernel(tc, z, G2, out):
     nc = tc.nc
     with ExitStack() as ctx:
         keep = ctx.enter_context(tc.tile_pool(name="keep", bufs=1))
-        work = ctx.enter_context(tc.tile_pool(name="work", bufs=2))
+        work = ctx.enter_context(tc.tile_pool(name="work", bufs=4))
         psum_once = ctx.enter_context(tc.psum_pool(name="psum_once", bufs=1))
         psum_turn = ctx.enter_context(tc.psum_pool(name="psum_turn", bufs=3))
         psum_acc = ctx.enter_context(tc.psum_pool(name="psum_acc", bufs=3))
@@ -50,10 +51,9 @@ def tile_fast_tucker_taylor_pa_s_kernel(tc, z, G2, out):
         zT_ps = psum_once.tile([P, ORD, P], BF16)
         for i in range(ORD):
             nc.tensor.transpose(out=zT_ps[:, i, :], in_=z_rows[:, i, :], identity=ident_bf16[:])
+        zT_bank = zT_ps[:].rearrange("s i (a j) -> s i j a", j=N_TILES)
         zT = keep.tile([P, ORD, N_TILES, R], F32)
-        nc.vector.tensor_copy(
-            out=zT[:], in_=zT_ps[:].rearrange("s i (a j) -> s i j a", j=N_TILES)
-        )
+        nc.scalar.copy(out=zT[:], in_=zT_bank)
 
         g_words = g_rows[:].bitcast(F32).rearrange("m h (q u) -> m h q u", u=PAIRS)
         gT_ps = psum_once.tile([P, M_TILES, PAIRS, P], F32)
@@ -70,26 +70,35 @@ def tile_fast_tucker_taylor_pa_s_kernel(tc, z, G2, out):
         g_codes = keep.tile([P, M], U32, align_bytes=64)
         g_scales = keep.tile([P, M], U8, align_bytes=64)
 
+        out_by_half = out.rearrange("(h m) n -> m h n", m=P)
         kronT_of = {}
         grouped_of = {}
 
         def multiply(g):
-            tiles = slice(g * CHUNK_TILES, (g + 1) * CHUNK_TILES)
-            pair = work.tile([P, CHUNK_TILES, R, R], F32)
+            tiles = slice(g * UNIT_TILES, (g + 1) * UNIT_TILES)
+            pair = work.tile([P, UNIT_TILES, R, R], F32)
             nc.vector.tensor_tensor(
                 out=pair[:],
-                in0=zT[:, 0, tiles, :].unsqueeze(2).to_broadcast([P, CHUNK_TILES, R, R]),
-                in1=zT[:, 1, tiles, :].unsqueeze(3).to_broadcast([P, CHUNK_TILES, R, R]),
+                in0=zT_bank[:, 0, tiles, :].unsqueeze(2).to_broadcast([P, UNIT_TILES, R, R]),
+                in1=zT[:, 1, tiles, :].unsqueeze(3).to_broadcast([P, UNIT_TILES, R, R]),
                 op=MULT,
             )
-            kronT = work.tile([P, CHUNK_TILES, R, R * R], BF16)
+            pair_flat = pair[:].rearrange("s j b a -> s j (b a)").unsqueeze(2)
+            kronT = work.tile([P, UNIT_TILES, R, R * R], BF16)
             nc.vector.tensor_tensor(
-                out=kronT[:],
-                in0=pair[:]
-                .rearrange("s j b a -> s j (b a)")
-                .unsqueeze(2)
-                .to_broadcast([P, CHUNK_TILES, R, R * R]),
-                in1=zT[:, 2, tiles, :].unsqueeze(3).to_broadcast([P, CHUNK_TILES, R, R * R]),
+                out=kronT[:, :, :C_VECTOR, :],
+                in0=pair_flat.to_broadcast([P, UNIT_TILES, C_VECTOR, R * R]),
+                in1=zT_bank[:, 2, tiles, :C_VECTOR]
+                .unsqueeze(3)
+                .to_broadcast([P, UNIT_TILES, C_VECTOR, R * R]),
+                op=MULT,
+            )
+            nc.gpsimd.tensor_tensor(
+                out=kronT[:, :, C_VECTOR:, :],
+                in0=pair_flat.to_broadcast([P, UNIT_TILES, C_POOL, R * R]),
+                in1=zT[:, 2, tiles, C_VECTOR:]
+                .unsqueeze(3)
+                .to_broadcast([P, UNIT_TILES, C_POOL, R * R]),
                 op=MULT,
             )
             kronT_of[g] = kronT
@@ -101,36 +110,32 @@ def tile_fast_tucker_taylor_pa_s_kernel(tc, z, G2, out):
                 .bitcast(F32)
                 .rearrange("s j (q u) -> s j q u", u=PAIRS)
             )
-            grouped = work.tile([P, CHUNK * PACK], BF16, align_bytes=64)
-            grouped_words = grouped[:].bitcast(F32).rearrange(
-                "q (j s u) -> q j s u", j=CHUNK_TILES, u=PAIRS
+            turned = psum_turn.tile([P, UNIT_TILES, PAIRS, P], F32)
+            for j in range(UNIT_TILES):
+                for u in range(PAIRS):
+                    nc.tensor.transpose(
+                        out=turned[:, j, u, :], in_=words[:, j, :, u], identity=ident_f32[:]
+                    )
+            grouped = work.tile([P, UNIT * PACK], BF16, align_bytes=64)
+            nc.scalar.copy(
+                out=grouped[:]
+                .bitcast(F32)
+                .rearrange("q (j s u) -> q j s u", j=UNIT_TILES, u=PAIRS),
+                in_=turned[:].rearrange("q j u s -> q j s u"),
             )
-            for first in range(0, CHUNK_TILES, BANK_TILES):
-                turned = psum_turn.tile([P, BANK_TILES, PAIRS, P], F32)
-                for t in range(BANK_TILES):
-                    for u in range(PAIRS):
-                        nc.tensor.transpose(
-                            out=turned[:, t, u, :],
-                            in_=words[:, first + t, :, u],
-                            identity=ident_f32[:],
-                        )
-                nc.scalar.copy(
-                    out=grouped_words[:, first : first + BANK_TILES, :, :],
-                    in_=turned[:].rearrange("q t u s -> q t s u"),
-                )
             grouped_of[g] = grouped
 
         def contract(g):
-            k_codes = work.tile([P, CHUNK], U32, align_bytes=64)
-            k_scales = work.tile([P, CHUNK], U8, align_bytes=64)
+            k_codes = work.tile([P, UNIT], U32, align_bytes=64)
+            k_scales = work.tile([P, UNIT], U8, align_bytes=64)
             nc.vector.quantize_mx(
                 out=k_codes[:].bitcast(FP8X4), scales=k_scales[:], in_=grouped_of[g][:]
             )
+            acc = psum_acc.tile([P, M_TILES, UNIT], F32)
             for h in range(M_TILES):
                 rows = slice(h * P, (h + 1) * P)
-                acc = psum_acc.tile([P, CHUNK], F32)
                 nc.tensor.matmul_mx(
-                    out=acc[:],
+                    out=acc[:, h, :],
                     lhsT=g_codes[:, rows].bitcast(FP8X4),
                     lhsT_scale=g_scales[:, rows],
                     rhs=k_codes[:].bitcast(FP8X4),
@@ -138,19 +143,18 @@ def tile_fast_tucker_taylor_pa_s_kernel(tc, z, G2, out):
                     start=True,
                     stop=True,
                 )
-                result = work.tile([P, CHUNK], F32, bufs=4)
-                nc.scalar.copy(out=result[:], in_=acc[:])
-                nc.sync.dma_start(out=out[rows, g * CHUNK : (g + 1) * CHUNK], in_=result[:])
+            result = work.tile([P, M_TILES, UNIT], F32)
+            nc.scalar.copy(out=result[:], in_=acc[:])
+            nc.sync.dma_start(out=out_by_half[:, :, g * UNIT : (g + 1) * UNIT], in_=result[:])
 
-        multiply(0)
-        nc.vector.quantize_mx(
-            out=g_codes[:].bitcast(FP8X4), scales=g_scales[:], in_=g_grouped[:]
-        )
-        turn(0)
-        multiply(1)
-        for g in range(CHUNKS):
-            if g + 1 < CHUNKS:
-                turn(g + 1)
-            contract(g)
-            if g + 2 < CHUNKS:
-                multiply(g + 2)
+        for step in range(UNITS + 2):
+            if step < UNITS:
+                multiply(step)
+            if step == 1:
+                nc.vector.quantize_mx(
+                    out=g_codes[:].bitcast(FP8X4), scales=g_scales[:], in_=g_grouped[:]
+                )
+            if 1 <= step <= UNITS:
+                turn(step - 1)
+            if step >= 2:
+                contract(step - 2)

@@ -23,8 +23,7 @@ M_TILES = M // P
 UNIT_TILES = 2
 UNIT = UNIT_TILES * P
 UNITS = N_TILES // UNIT_TILES
-C_POOL = 3
-C_VECTOR = R - C_POOL
+QUANTISE_LAG = 2
 
 FLOPS = 2 * M * K * N
 
@@ -33,10 +32,11 @@ def tile_fast_tucker_taylor_pa_s_kernel(tc, z, G2, out):
     nc = tc.nc
     with ExitStack() as ctx:
         keep = ctx.enter_context(tc.tile_pool(name="keep", bufs=1))
-        work = ctx.enter_context(tc.tile_pool(name="work", bufs=4))
+        work = ctx.enter_context(tc.tile_pool(name="work", bufs=5))
         psum_once = ctx.enter_context(tc.psum_pool(name="psum_once", bufs=1))
         psum_turn = ctx.enter_context(tc.psum_pool(name="psum_turn", bufs=3))
         psum_acc = ctx.enter_context(tc.psum_pool(name="psum_acc", bufs=3))
+        ctx.enter_context(tc.manual_schedule())
 
         z_rows = keep.tile([P, ORD, P], BF16)
         nc.sync.dma_start(out=z_rows[:], in_=z.rearrange("i a (j s) -> (a j) i s", s=P))
@@ -51,9 +51,10 @@ def tile_fast_tucker_taylor_pa_s_kernel(tc, z, G2, out):
         zT_ps = psum_once.tile([P, ORD, P], BF16)
         for i in range(ORD):
             nc.tensor.transpose(out=zT_ps[:, i, :], in_=z_rows[:, i, :], identity=ident_bf16[:])
-        zT_bank = zT_ps[:].rearrange("s i (a j) -> s i j a", j=N_TILES)
         zT = keep.tile([P, ORD, N_TILES, R], F32)
-        nc.scalar.copy(out=zT[:], in_=zT_bank)
+        nc.vector.tensor_copy(
+            out=zT[:], in_=zT_ps[:].rearrange("s i (a j) -> s i j a", j=N_TILES)
+        )
 
         g_words = g_rows[:].bitcast(F32).rearrange("m h (q u) -> m h q u", u=PAIRS)
         gT_ps = psum_once.tile([P, M_TILES, PAIRS, P], F32)
@@ -71,34 +72,31 @@ def tile_fast_tucker_taylor_pa_s_kernel(tc, z, G2, out):
         g_scales = keep.tile([P, M], U8, align_bytes=64)
 
         out_by_half = out.rearrange("(h m) n -> m h n", m=P)
+        pair_of = {}
         kronT_of = {}
         grouped_of = {}
 
-        def multiply(g):
+        def multiply_two(g):
             tiles = slice(g * UNIT_TILES, (g + 1) * UNIT_TILES)
             pair = work.tile([P, UNIT_TILES, R, R], F32)
             nc.vector.tensor_tensor(
                 out=pair[:],
-                in0=zT_bank[:, 0, tiles, :].unsqueeze(2).to_broadcast([P, UNIT_TILES, R, R]),
+                in0=zT[:, 0, tiles, :].unsqueeze(2).to_broadcast([P, UNIT_TILES, R, R]),
                 in1=zT[:, 1, tiles, :].unsqueeze(3).to_broadcast([P, UNIT_TILES, R, R]),
                 op=MULT,
             )
-            pair_flat = pair[:].rearrange("s j b a -> s j (b a)").unsqueeze(2)
+            pair_of[g] = pair
+
+        def multiply_third(g):
+            tiles = slice(g * UNIT_TILES, (g + 1) * UNIT_TILES)
             kronT = work.tile([P, UNIT_TILES, R, R * R], BF16)
             nc.vector.tensor_tensor(
-                out=kronT[:, :, :C_VECTOR, :],
-                in0=pair_flat.to_broadcast([P, UNIT_TILES, C_VECTOR, R * R]),
-                in1=zT_bank[:, 2, tiles, :C_VECTOR]
-                .unsqueeze(3)
-                .to_broadcast([P, UNIT_TILES, C_VECTOR, R * R]),
-                op=MULT,
-            )
-            nc.gpsimd.tensor_tensor(
-                out=kronT[:, :, C_VECTOR:, :],
-                in0=pair_flat.to_broadcast([P, UNIT_TILES, C_POOL, R * R]),
-                in1=zT[:, 2, tiles, C_VECTOR:]
-                .unsqueeze(3)
-                .to_broadcast([P, UNIT_TILES, C_POOL, R * R]),
+                out=kronT[:],
+                in0=pair_of[g][:]
+                .rearrange("s j b a -> s j (b a)")
+                .unsqueeze(2)
+                .to_broadcast([P, UNIT_TILES, R, R * R]),
+                in1=zT[:, 2, tiles, :].unsqueeze(3).to_broadcast([P, UNIT_TILES, R, R * R]),
                 op=MULT,
             )
             kronT_of[g] = kronT
@@ -147,14 +145,15 @@ def tile_fast_tucker_taylor_pa_s_kernel(tc, z, G2, out):
             nc.scalar.copy(out=result[:], in_=acc[:])
             nc.sync.dma_start(out=out_by_half[:, :, g * UNIT : (g + 1) * UNIT], in_=result[:])
 
-        for step in range(UNITS + 2):
+        for step in range(UNITS + 1 + QUANTISE_LAG):
             if step < UNITS:
-                multiply(step)
-            if step == 1:
+                multiply_two(step)
+            if 1 <= step <= UNITS:
+                multiply_third(step - 1)
+                turn(step - 1)
+            if step == QUANTISE_LAG:
                 nc.vector.quantize_mx(
                     out=g_codes[:].bitcast(FP8X4), scales=g_scales[:], in_=g_grouped[:]
                 )
-            if 1 <= step <= UNITS:
-                turn(step - 1)
-            if step >= 2:
-                contract(step - 2)
+            if step >= 1 + QUANTISE_LAG:
+                contract(step - 1 - QUANTISE_LAG)

@@ -23,7 +23,8 @@ M_TILES = M // P
 UNIT_TILES = 2
 UNIT = UNIT_TILES * P
 UNITS = N_TILES // UNIT_TILES
-QUANTISE_LAG = 2
+SCALAR_C = (2, 1, 2, 1, 2, 1, 2, 1)
+COPY = mybir.ActivationFunctionType.Copy
 
 FLOPS = 2 * M * K * N
 
@@ -64,10 +65,6 @@ def tile_fast_tucker_taylor_pa_s_kernel(tc, z, G2, out):
                     out=gT_ps[:, h, u, :], in_=g_words[:, h, :, u], identity=ident_f32[:]
                 )
         g_grouped = keep.tile([P, M * PACK], BF16, align_bytes=64)
-        nc.scalar.copy(
-            out=g_grouped[:].bitcast(F32).rearrange("q (h m u) -> q h m u", h=M_TILES, u=PAIRS),
-            in_=gT_ps[:].rearrange("q h u m -> q h m u"),
-        )
         g_codes = keep.tile([P, M], U32, align_bytes=64)
         g_scales = keep.tile([P, M], U8, align_bytes=64)
 
@@ -75,6 +72,8 @@ def tile_fast_tucker_taylor_pa_s_kernel(tc, z, G2, out):
         pair_of = {}
         kronT_of = {}
         grouped_of = {}
+        turned_of = {}
+        codes_of = {}
 
         def multiply_two(g):
             tiles = slice(g * UNIT_TILES, (g + 1) * UNIT_TILES)
@@ -87,19 +86,30 @@ def tile_fast_tucker_taylor_pa_s_kernel(tc, z, G2, out):
             )
             pair_of[g] = pair
 
-        def multiply_third(g):
-            tiles = slice(g * UNIT_TILES, (g + 1) * UNIT_TILES)
+        def multiply_third_scalar(g):
             kronT = work.tile([P, UNIT_TILES, R, R * R], BF16)
+            kronT_of[g] = kronT
+            for j in range(UNIT_TILES):
+                for c in range(R - SCALAR_C[g], R):
+                    nc.scalar.activation(
+                        out=kronT[:, j, c, :],
+                        in_=pair_of[g][:, j, :, :].rearrange("s b a -> s (b a)"),
+                        func=COPY,
+                        scale=zT[:, 2, g * UNIT_TILES + j, c : c + 1],
+                    )
+
+        def multiply_third_vector(g):
+            tiles = slice(g * UNIT_TILES, (g + 1) * UNIT_TILES)
+            cs = R - SCALAR_C[g]
             nc.vector.tensor_tensor(
-                out=kronT[:],
+                out=kronT_of[g][:, :, 0:cs, :],
                 in0=pair_of[g][:]
                 .rearrange("s j b a -> s j (b a)")
                 .unsqueeze(2)
-                .to_broadcast([P, UNIT_TILES, R, R * R]),
-                in1=zT[:, 2, tiles, :].unsqueeze(3).to_broadcast([P, UNIT_TILES, R, R * R]),
+                .to_broadcast([P, UNIT_TILES, cs, R * R]),
+                in1=zT[:, 2, tiles, 0:cs].unsqueeze(3).to_broadcast([P, UNIT_TILES, cs, R * R]),
                 op=MULT,
             )
-            kronT_of[g] = kronT
 
         def turn(g):
             words = (
@@ -114,21 +124,28 @@ def tile_fast_tucker_taylor_pa_s_kernel(tc, z, G2, out):
                     nc.tensor.transpose(
                         out=turned[:, j, u, :], in_=words[:, j, :, u], identity=ident_f32[:]
                     )
+            turned_of[g] = turned
+
+        def regroup(g):
             grouped = work.tile([P, UNIT * PACK], BF16, align_bytes=64)
             nc.scalar.copy(
                 out=grouped[:]
                 .bitcast(F32)
                 .rearrange("q (j s u) -> q j s u", j=UNIT_TILES, u=PAIRS),
-                in_=turned[:].rearrange("q j u s -> q j s u"),
+                in_=turned_of[g][:].rearrange("q j u s -> q j s u"),
             )
             grouped_of[g] = grouped
 
-        def contract(g):
+        def quantise(g):
             k_codes = work.tile([P, UNIT], U32, align_bytes=64)
             k_scales = work.tile([P, UNIT], U8, align_bytes=64)
             nc.vector.quantize_mx(
                 out=k_codes[:].bitcast(FP8X4), scales=k_scales[:], in_=grouped_of[g][:]
             )
+            codes_of[g] = (k_codes, k_scales)
+
+        def product(g):
+            k_codes, k_scales = codes_of[g]
             acc = psum_acc.tile([P, M_TILES, UNIT], F32)
             for h in range(M_TILES):
                 rows = slice(h * P, (h + 1) * P)
@@ -145,15 +162,27 @@ def tile_fast_tucker_taylor_pa_s_kernel(tc, z, G2, out):
             nc.scalar.copy(out=result[:], in_=acc[:])
             nc.sync.dma_start(out=out_by_half[:, :, g * UNIT : (g + 1) * UNIT], in_=result[:])
 
-        for step in range(UNITS + 1 + QUANTISE_LAG):
+        for step in range(UNITS + 4):
             if step < UNITS:
                 multiply_two(step)
-            if 1 <= step <= UNITS:
-                multiply_third(step - 1)
+                multiply_third_scalar(step)
+            if step == 1:
+                nc.scalar.copy(
+                    out=g_grouped[:]
+                    .bitcast(F32)
+                    .rearrange("q (h m u) -> q h m u", h=M_TILES, u=PAIRS),
+                    in_=gT_ps[:].rearrange("q h u m -> q h m u"),
+                )
+            if 0 <= step - 2 < UNITS:
+                regroup(step - 2)
+            if 0 <= step - 4 < UNITS:
+                product(step - 4)
+            if 0 <= step - 1 < UNITS:
+                multiply_third_vector(step - 1)
                 turn(step - 1)
-            if step == QUANTISE_LAG:
+            if step == 2:
                 nc.vector.quantize_mx(
                     out=g_codes[:].bitcast(FP8X4), scales=g_scales[:], in_=g_grouped[:]
                 )
-            if step >= 1 + QUANTISE_LAG:
-                contract(step - 1 - QUANTISE_LAG)
+            if 0 <= step - 3 < UNITS:
+                quantise(step - 3)

@@ -23,7 +23,10 @@ M_TILES = M // P
 UNIT_TILES = 2
 UNIT = UNIT_TILES * P
 UNITS = N_TILES // UNIT_TILES
-SCALAR_C = (2, 1, 2, 1, 2, 1, 2, 1)
+VECTOR_C = 5
+GPSIMD_C = 2
+SCALAR_C = 1
+ADD = mybir.AluOpType.add
 COPY = mybir.ActivationFunctionType.Copy
 
 FLOPS = 2 * M * K * N
@@ -52,10 +55,9 @@ def tile_fast_tucker_taylor_pa_s_kernel(tc, z, G2, out):
         zT_ps = psum_once.tile([P, ORD, P], BF16)
         for i in range(ORD):
             nc.tensor.transpose(out=zT_ps[:, i, :], in_=z_rows[:, i, :], identity=ident_bf16[:])
+        zT_ps_by_tile = zT_ps[:].rearrange("s i (a j) -> s i j a", j=N_TILES)
         zT = keep.tile([P, ORD, N_TILES, R], F32)
-        nc.vector.tensor_copy(
-            out=zT[:], in_=zT_ps[:].rearrange("s i (a j) -> s i j a", j=N_TILES)
-        )
+        nc.vector.tensor_copy(out=zT[:], in_=zT_ps_by_tile)
 
         g_words = g_rows[:].bitcast(F32).rearrange("m h (q u) -> m h q u", u=PAIRS)
         gT_ps = psum_once.tile([P, M_TILES, PAIRS, P], F32)
@@ -80,7 +82,7 @@ def tile_fast_tucker_taylor_pa_s_kernel(tc, z, G2, out):
             pair = work.tile([P, UNIT_TILES, R, R], F32)
             nc.vector.tensor_tensor(
                 out=pair[:],
-                in0=zT[:, 0, tiles, :].unsqueeze(2).to_broadcast([P, UNIT_TILES, R, R]),
+                in0=zT_ps_by_tile[:, 0, tiles, :].unsqueeze(2).to_broadcast([P, UNIT_TILES, R, R]),
                 in1=zT[:, 1, tiles, :].unsqueeze(3).to_broadcast([P, UNIT_TILES, R, R]),
                 op=MULT,
             )
@@ -90,7 +92,16 @@ def tile_fast_tucker_taylor_pa_s_kernel(tc, z, G2, out):
             kronT = work.tile([P, UNIT_TILES, R, R * R], BF16)
             kronT_of[g] = kronT
             for j in range(UNIT_TILES):
-                for c in range(R - SCALAR_C[g], R):
+                for c in range(VECTOR_C, VECTOR_C + GPSIMD_C):
+                    nc.gpsimd.tensor_scalar(
+                        out=kronT[:, j, c, :],
+                        in0=pair_of[g][:, j, :, :].rearrange("s b a -> s (b a)"),
+                        scalar1=zT[:, 2, g * UNIT_TILES + j, c : c + 1],
+                        scalar2=0.0,
+                        op0=MULT,
+                        op1=ADD,
+                    )
+                for c in range(R - SCALAR_C, R):
                     nc.scalar.activation(
                         out=kronT[:, j, c, :],
                         in_=pair_of[g][:, j, :, :].rearrange("s b a -> s (b a)"),
@@ -100,14 +111,16 @@ def tile_fast_tucker_taylor_pa_s_kernel(tc, z, G2, out):
 
         def multiply_third_vector(g):
             tiles = slice(g * UNIT_TILES, (g + 1) * UNIT_TILES)
-            cs = R - SCALAR_C[g]
+            cs = VECTOR_C
             nc.vector.tensor_tensor(
                 out=kronT_of[g][:, :, 0:cs, :],
                 in0=pair_of[g][:]
                 .rearrange("s j b a -> s j (b a)")
                 .unsqueeze(2)
                 .to_broadcast([P, UNIT_TILES, cs, R * R]),
-                in1=zT[:, 2, tiles, 0:cs].unsqueeze(3).to_broadcast([P, UNIT_TILES, cs, R * R]),
+                in1=zT_ps_by_tile[:, 2, tiles, 0:cs]
+                .unsqueeze(3)
+                .to_broadcast([P, UNIT_TILES, cs, R * R]),
                 op=MULT,
             )
 

@@ -20,13 +20,11 @@ N = 2048
 M = 256
 N_TILES = N // P
 M_TILES = M // P
-UNIT_TILES = 2
-UNIT = UNIT_TILES * P
-UNITS = N_TILES // UNIT_TILES
-VECTOR_C = 5
-GPSIMD_C = 2
-SCALAR_C = 1
-ADD = mybir.AluOpType.add
+UNIT_TILES = (2, 2, 2, 2, 2, 2, 2, 2)
+UNITS = len(UNIT_TILES)
+SCALAR_C = (3, 2, 1, 0, 1, 0, 1, 0)
+VECTOR_COPIES = ()
+PAIR_RUNS = ((0, 2, False), (2, 2, False), (4, 4, True), (8, 8, True))
 COPY = mybir.ActivationFunctionType.Copy
 
 FLOPS = 2 * M * K * N
@@ -34,6 +32,7 @@ FLOPS = 2 * M * K * N
 
 def tile_fast_tucker_taylor_pa_s_kernel(tc, z, G2, out):
     nc = tc.nc
+    FIRST_TILE = [sum(UNIT_TILES[:g]) for g in range(UNITS)]
     with ExitStack() as ctx:
         keep = ctx.enter_context(tc.tile_pool(name="keep", bufs=1))
         work = ctx.enter_context(tc.tile_pool(name="work", bufs=5))
@@ -59,6 +58,32 @@ def tile_fast_tucker_taylor_pa_s_kernel(tc, z, G2, out):
         zT = keep.tile([P, ORD, N_TILES, R], F32)
         nc.vector.tensor_copy(out=zT[:], in_=zT_ps_by_tile)
 
+        pair_of_tile = {}
+        for first, tiles, on_gpsimd in PAIR_RUNS:
+            run = slice(first, first + tiles)
+            pair = keep.tile([P, tiles, R, R], F32, name="pair%d" % first)
+            z1 = zT[:, 1, run, :].unsqueeze(3).to_broadcast([P, tiles, R, R])
+            if on_gpsimd:
+                nc.gpsimd.tensor_tensor(
+                    out=pair[:],
+                    in0=zT[:, 0, run, :].unsqueeze(2).to_broadcast([P, tiles, R, R]),
+                    in1=z1,
+                    op=MULT,
+                )
+            else:
+                nc.vector.tensor_tensor(
+                    out=pair[:],
+                    in0=zT_ps_by_tile[:, 0, run, :].unsqueeze(2).to_broadcast([P, tiles, R, R]),
+                    in1=z1,
+                    op=MULT,
+                )
+            for j in range(tiles):
+                pair_of_tile[first + j] = (pair, j)
+
+        def pair_view(g):
+            pair, j = pair_of_tile[FIRST_TILE[g]]
+            return pair[:, j : j + UNIT_TILES[g], :, :].rearrange("s j b a -> s j (b a)")
+
         g_words = g_rows[:].bitcast(F32).rearrange("m h (q u) -> m h q u", u=PAIRS)
         gT_ps = psum_once.tile([P, M_TILES, PAIRS, P], F32)
         for h in range(M_TILES):
@@ -71,56 +96,30 @@ def tile_fast_tucker_taylor_pa_s_kernel(tc, z, G2, out):
         g_scales = keep.tile([P, M], U8, align_bytes=64)
 
         out_by_half = out.rearrange("(h m) n -> m h n", m=P)
-        pair_of = {}
         kronT_of = {}
-        grouped_of = {}
         turned_of = {}
+        grouped_of = {}
         codes_of = {}
 
-        def multiply_two(g):
-            tiles = slice(g * UNIT_TILES, (g + 1) * UNIT_TILES)
-            pair = work.tile([P, UNIT_TILES, R, R], F32)
-            nc.vector.tensor_tensor(
-                out=pair[:],
-                in0=zT_ps_by_tile[:, 0, tiles, :].unsqueeze(2).to_broadcast([P, UNIT_TILES, R, R]),
-                in1=zT[:, 1, tiles, :].unsqueeze(3).to_broadcast([P, UNIT_TILES, R, R]),
-                op=MULT,
-            )
-            pair_of[g] = pair
-
         def multiply_third_scalar(g):
-            kronT = work.tile([P, UNIT_TILES, R, R * R], BF16)
+            kronT = work.tile([P, UNIT_TILES[g], R, R * R], BF16, name="kronT")
             kronT_of[g] = kronT
-            for j in range(UNIT_TILES):
-                for c in range(VECTOR_C, VECTOR_C + GPSIMD_C):
-                    nc.gpsimd.tensor_scalar(
-                        out=kronT[:, j, c, :],
-                        in0=pair_of[g][:, j, :, :].rearrange("s b a -> s (b a)"),
-                        scalar1=zT[:, 2, g * UNIT_TILES + j, c : c + 1],
-                        scalar2=0.0,
-                        op0=MULT,
-                        op1=ADD,
-                    )
-                for c in range(R - SCALAR_C, R):
+            for j in range(UNIT_TILES[g]):
+                for c in range(R - SCALAR_C[g], R):
                     nc.scalar.activation(
                         out=kronT[:, j, c, :],
-                        in_=pair_of[g][:, j, :, :].rearrange("s b a -> s (b a)"),
+                        in_=pair_view(g)[:, j, :],
                         func=COPY,
-                        scale=zT[:, 2, g * UNIT_TILES + j, c : c + 1],
+                        scale=zT[:, 2, FIRST_TILE[g] + j, c : c + 1],
                     )
 
         def multiply_third_vector(g):
-            tiles = slice(g * UNIT_TILES, (g + 1) * UNIT_TILES)
-            cs = VECTOR_C
+            tiles = slice(FIRST_TILE[g], FIRST_TILE[g] + UNIT_TILES[g])
+            shape = [P, UNIT_TILES[g], R - SCALAR_C[g], R * R]
             nc.vector.tensor_tensor(
-                out=kronT_of[g][:, :, 0:cs, :],
-                in0=pair_of[g][:]
-                .rearrange("s j b a -> s j (b a)")
-                .unsqueeze(2)
-                .to_broadcast([P, UNIT_TILES, cs, R * R]),
-                in1=zT_ps_by_tile[:, 2, tiles, 0:cs]
-                .unsqueeze(3)
-                .to_broadcast([P, UNIT_TILES, cs, R * R]),
+                out=kronT_of[g][:, :, 0 : R - SCALAR_C[g], :],
+                in0=pair_view(g).unsqueeze(2).to_broadcast(shape),
+                in1=zT_ps_by_tile[:, 2, tiles, 0 : R - SCALAR_C[g]].unsqueeze(3).to_broadcast(shape),
                 op=MULT,
             )
 
@@ -131,27 +130,32 @@ def tile_fast_tucker_taylor_pa_s_kernel(tc, z, G2, out):
                 .bitcast(F32)
                 .rearrange("s j (q u) -> s j q u", u=PAIRS)
             )
-            turned = psum_turn.tile([P, UNIT_TILES, PAIRS, P], F32)
-            for j in range(UNIT_TILES):
+            turned = psum_turn.tile([P, UNIT_TILES[g], PAIRS, P], F32, name="turned")
+            for j in range(UNIT_TILES[g]):
                 for u in range(PAIRS):
                     nc.tensor.transpose(
                         out=turned[:, j, u, :], in_=words[:, j, :, u], identity=ident_f32[:]
                     )
             turned_of[g] = turned
 
+        def copy_out(g, out_ap, in_ap):
+            if g in VECTOR_COPIES:
+                nc.vector.tensor_copy(out=out_ap, in_=in_ap)
+            else:
+                nc.scalar.copy(out=out_ap, in_=in_ap)
+
         def regroup(g):
-            grouped = work.tile([P, UNIT * PACK], BF16, align_bytes=64)
-            nc.scalar.copy(
-                out=grouped[:]
-                .bitcast(F32)
-                .rearrange("q (j s u) -> q j s u", j=UNIT_TILES, u=PAIRS),
-                in_=turned_of[g][:].rearrange("q j u s -> q j s u"),
+            grouped = work.tile([P, UNIT_TILES[g] * P * PACK], BF16, align_bytes=64, name="grouped")
+            copy_out(
+                g,
+                grouped[:].bitcast(F32).rearrange("q (j s u) -> q j s u", j=UNIT_TILES[g], u=PAIRS),
+                turned_of[g][:].rearrange("q j u s -> q j s u"),
             )
             grouped_of[g] = grouped
 
         def quantise(g):
-            k_codes = work.tile([P, UNIT], U32, align_bytes=64)
-            k_scales = work.tile([P, UNIT], U8, align_bytes=64)
+            k_codes = work.tile([P, UNIT_TILES[g] * P], U32, align_bytes=64, name="k_codes")
+            k_scales = work.tile([P, UNIT_TILES[g] * P], U8, align_bytes=64, name="k_scales")
             nc.vector.quantize_mx(
                 out=k_codes[:].bitcast(FP8X4), scales=k_scales[:], in_=grouped_of[g][:]
             )
@@ -159,7 +163,8 @@ def tile_fast_tucker_taylor_pa_s_kernel(tc, z, G2, out):
 
         def product(g):
             k_codes, k_scales = codes_of[g]
-            acc = psum_acc.tile([P, M_TILES, UNIT], F32)
+            width = UNIT_TILES[g] * P
+            acc = psum_acc.tile([P, M_TILES, width], F32, name="acc")
             for h in range(M_TILES):
                 rows = slice(h * P, (h + 1) * P)
                 nc.tensor.matmul_mx(
@@ -171,13 +176,13 @@ def tile_fast_tucker_taylor_pa_s_kernel(tc, z, G2, out):
                     start=True,
                     stop=True,
                 )
-            result = work.tile([P, M_TILES, UNIT], F32)
-            nc.scalar.copy(out=result[:], in_=acc[:])
-            nc.sync.dma_start(out=out_by_half[:, :, g * UNIT : (g + 1) * UNIT], in_=result[:])
+            result = work.tile([P, M_TILES, width], F32, name="result")
+            copy_out(g, result[:], acc[:])
+            first = FIRST_TILE[g] * P
+            nc.sync.dma_start(out=out_by_half[:, :, first : first + width], in_=result[:])
 
         for step in range(UNITS + 4):
             if step < UNITS:
-                multiply_two(step)
                 multiply_third_scalar(step)
             if step == 1:
                 nc.scalar.copy(

@@ -20,11 +20,11 @@ N = 2048
 M = 256
 N_TILES = N // P
 M_TILES = M // P
-UNIT_TILES = (2, 2, 2, 2, 2, 2, 2, 2)
+UNIT_TILES = (2, 2, 2, 2, 2, 2, 2, 1, 1)
 UNITS = len(UNIT_TILES)
-SCALAR_C = (3, 2, 1, 0, 1, 0, 1, 0)
-VECTOR_COPIES = ()
-PAIR_RUNS = ((0, 2, False), (2, 2, False), (4, 4, True), (8, 8, True))
+SCALAR_C = (3, 2, 1, 0, 1, 0, 1, 0, 0)
+VECTOR_RESULTS = (5, 8)
+PAIR_RUNS = ((0, 4, False), (4, 4, True), (8, 8, True))
 COPY = mybir.ActivationFunctionType.Copy
 
 FLOPS = 2 * M * K * N
@@ -55,26 +55,32 @@ def tile_fast_tucker_taylor_pa_s_kernel(tc, z, G2, out):
         for i in range(ORD):
             nc.tensor.transpose(out=zT_ps[:, i, :], in_=z_rows[:, i, :], identity=ident_bf16[:])
         zT_ps_by_tile = zT_ps[:].rearrange("s i (a j) -> s i j a", j=N_TILES)
+        z1_first = keep.tile([P, PAIR_RUNS[0][1], R], F32)
+        nc.vector.tensor_copy(out=z1_first[:], in_=zT_ps_by_tile[:, 1, 0 : PAIR_RUNS[0][1], :])
+        zT_ps_again = psum_turn.tile([P, ORD, P], BF16, name="turned")
+        for i in range(ORD):
+            nc.tensor.transpose(
+                out=zT_ps_again[:, i, :], in_=z_rows[:, i, :], identity=ident_bf16[:]
+            )
         zT = keep.tile([P, ORD, N_TILES, R], F32)
-        nc.vector.tensor_copy(out=zT[:], in_=zT_ps_by_tile)
+        nc.scalar.copy(out=zT[:], in_=zT_ps_again[:].rearrange("s i (a j) -> s i j a", j=N_TILES))
 
         pair_of_tile = {}
         for first, tiles, on_gpsimd in PAIR_RUNS:
             run = slice(first, first + tiles)
             pair = keep.tile([P, tiles, R, R], F32, name="pair%d" % first)
-            z1 = zT[:, 1, run, :].unsqueeze(3).to_broadcast([P, tiles, R, R])
             if on_gpsimd:
                 nc.gpsimd.tensor_tensor(
                     out=pair[:],
                     in0=zT[:, 0, run, :].unsqueeze(2).to_broadcast([P, tiles, R, R]),
-                    in1=z1,
+                    in1=zT[:, 1, run, :].unsqueeze(3).to_broadcast([P, tiles, R, R]),
                     op=MULT,
                 )
             else:
                 nc.vector.tensor_tensor(
                     out=pair[:],
                     in0=zT_ps_by_tile[:, 0, run, :].unsqueeze(2).to_broadcast([P, tiles, R, R]),
-                    in1=z1,
+                    in1=z1_first[:].unsqueeze(3).to_broadcast([P, tiles, R, R]),
                     op=MULT,
                 )
             for j in range(tiles):
@@ -100,6 +106,7 @@ def tile_fast_tucker_taylor_pa_s_kernel(tc, z, G2, out):
         turned_of = {}
         grouped_of = {}
         codes_of = {}
+        acc_of = {}
 
         def multiply_third_scalar(g):
             kronT = work.tile([P, UNIT_TILES[g], R, R * R], BF16, name="kronT")
@@ -138,18 +145,13 @@ def tile_fast_tucker_taylor_pa_s_kernel(tc, z, G2, out):
                     )
             turned_of[g] = turned
 
-        def copy_out(g, out_ap, in_ap):
-            if g in VECTOR_COPIES:
-                nc.vector.tensor_copy(out=out_ap, in_=in_ap)
-            else:
-                nc.scalar.copy(out=out_ap, in_=in_ap)
-
         def regroup(g):
             grouped = work.tile([P, UNIT_TILES[g] * P * PACK], BF16, align_bytes=64, name="grouped")
-            copy_out(
-                g,
-                grouped[:].bitcast(F32).rearrange("q (j s u) -> q j s u", j=UNIT_TILES[g], u=PAIRS),
-                turned_of[g][:].rearrange("q j u s -> q j s u"),
+            nc.scalar.copy(
+                out=grouped[:]
+                .bitcast(F32)
+                .rearrange("q (j s u) -> q j s u", j=UNIT_TILES[g], u=PAIRS),
+                in_=turned_of[g][:].rearrange("q j u s -> q j s u"),
             )
             grouped_of[g] = grouped
 
@@ -176,8 +178,15 @@ def tile_fast_tucker_taylor_pa_s_kernel(tc, z, G2, out):
                     start=True,
                     stop=True,
                 )
+            acc_of[g] = acc
+
+        def store(g):
+            width = UNIT_TILES[g] * P
             result = work.tile([P, M_TILES, width], F32, name="result")
-            copy_out(g, result[:], acc[:])
+            if g in VECTOR_RESULTS:
+                nc.vector.tensor_copy(out=result[:], in_=acc_of[g][:])
+            else:
+                nc.scalar.copy(out=result[:], in_=acc_of[g][:])
             first = FIRST_TILE[g] * P
             nc.sync.dma_start(out=out_by_half[:, :, first : first + width], in_=result[:])
 
@@ -195,6 +204,8 @@ def tile_fast_tucker_taylor_pa_s_kernel(tc, z, G2, out):
                 regroup(step - 2)
             if 0 <= step - 4 < UNITS:
                 product(step - 4)
+                if step - 4 not in VECTOR_RESULTS:
+                    store(step - 4)
             if 0 <= step - 1 < UNITS:
                 multiply_third_vector(step - 1)
                 turn(step - 1)
@@ -204,3 +215,5 @@ def tile_fast_tucker_taylor_pa_s_kernel(tc, z, G2, out):
                 )
             if 0 <= step - 3 < UNITS:
                 quantise(step - 3)
+            if step - 4 in VECTOR_RESULTS:
+                store(step - 4)

@@ -24,7 +24,7 @@ UNIT_TILES = (2, 2, 2, 2, 2, 2, 2, 1, 1)
 UNITS = len(UNIT_TILES)
 SCALAR_C = (3, 2, 1, 0, 1, 0, 1, 0, 0)
 VECTOR_RESULTS = (5, 8)
-PAIR_RUNS = ((0, 4, False), (4, 4, True), (8, 8, True))
+PAIR_RUNS = ((0, 6, False), (6, 10, True))
 COPY = mybir.ActivationFunctionType.Copy
 
 FLOPS = 2 * M * K * N
@@ -209,7 +209,7 @@ def tile_fast_tucker_taylor_pa_s_kernel(tc, z, G2, out):
             if 0 <= step - 1 < UNITS:
                 multiply_third_vector(step - 1)
                 turn(step - 1)
-            if step == 2:
+            if step == 3:
                 nc.vector.quantize_mx(
                     out=g_codes[:].bitcast(FP8X4), scales=g_scales[:], in_=g_grouped[:]
                 )

@@ -9,6 +9,7 @@ U32 = mybir.dt.uint32
 U8 = mybir.dt.uint8
 FP8X4 = mybir.dt.float8_e4m3fn_x4
 MULT = mybir.AluOpType.mult
+COPY = mybir.ActivationFunctionType.Copy
 
 P = 128
 ORD = 3
@@ -20,31 +21,48 @@ N = 2048
 M = 256
 N_TILES = N // P
 M_TILES = M // P
-UNIT_TILES = (2, 2, 2, 2, 2, 2, 2, 1, 1)
-UNITS = len(UNIT_TILES)
-SCALAR_C = (3, 2, 1, 0, 1, 0, 1, 0, 0)
-VECTOR_RESULTS = (5, 8)
-PAIR_RUNS = ((0, 6, False), (6, 10, True))
-COPY = mybir.ActivationFunctionType.Copy
+BANK = 512
+
+S_TILES = 8
+K_TILES = N_TILES - S_TILES
+K_FIRST = S_TILES * P
+UNITS = ((0, 256), (256, 256), (512, 256), (1024, 256), (1280, 256), (768, 256), (1536, 256), (1792, 128), (1920, 128))
+SCALAR_C = (2, 2, 2, 0, 0, 6, 0, 0, 0)
+SCALAR_STEP = (0, 0, 1, 0, 0, 4, 0, 0, 0)
+FIRST_QUANTISE = 4
+VECTOR_RESULTS = (8,)
+TURN_W_STEP = (2, 4)
 
 FLOPS = 2 * M * K * N
 
 
 def tile_fast_tucker_taylor_pa_s_kernel(tc, z, G2, out):
     nc = tc.nc
-    FIRST_TILE = [sum(UNIT_TILES[:g]) for g in range(UNITS)]
     with ExitStack() as ctx:
         keep = ctx.enter_context(tc.tile_pool(name="keep", bufs=1))
         work = ctx.enter_context(tc.tile_pool(name="work", bufs=5))
         psum_once = ctx.enter_context(tc.psum_pool(name="psum_once", bufs=1))
-        psum_turn = ctx.enter_context(tc.psum_pool(name="psum_turn", bufs=3))
+        psum_turn = ctx.enter_context(tc.psum_pool(name="psum_turn", bufs=2))
         psum_acc = ctx.enter_context(tc.psum_pool(name="psum_acc", bufs=3))
         ctx.enter_context(tc.manual_schedule())
 
         z_rows = keep.tile([P, ORD, P], BF16)
         nc.sync.dma_start(out=z_rows[:], in_=z.rearrange("i a (j s) -> (a j) i s", s=P))
         g_rows = keep.tile([P, M_TILES, K], BF16)
-        nc.sync.dma_start(out=g_rows[:], in_=G2.rearrange("(h m) k -> m h k", m=P))
+        z0_spread = []
+        for bank in range(K_TILES * P // BANK):
+            spread = keep.tile([P, PACK, BANK], BF16, name="z0_spread%d" % bank)
+            columns = slice(K_FIRST + bank * BANK, K_FIRST + (bank + 1) * BANK)
+            for half in range(2):
+                nc.sync.dma_start(
+                    out=spread[half::2, :, :],
+                    in_=z[0, PACK * half : PACK * (half + 1), columns]
+                    .unsqueeze(0)
+                    .to_broadcast([P // 2, PACK, BANK]),
+                )
+            z0_spread.append(spread)
+            if bank == 0:
+                nc.sync.dma_start(out=g_rows[:], in_=G2.rearrange("(h m) k -> m h k", m=P))
 
         ident_bf16 = keep.tile([P, P], BF16)
         make_identity(nc, ident_bf16[:])
@@ -54,44 +72,52 @@ def tile_fast_tucker_taylor_pa_s_kernel(tc, z, G2, out):
         zT_ps = psum_once.tile([P, ORD, P], BF16)
         for i in range(ORD):
             nc.tensor.transpose(out=zT_ps[:, i, :], in_=z_rows[:, i, :], identity=ident_bf16[:])
-        zT_ps_by_tile = zT_ps[:].rearrange("s i (a j) -> s i j a", j=N_TILES)
-        z1_first = keep.tile([P, PAIR_RUNS[0][1], R], F32)
-        nc.vector.tensor_copy(out=z1_first[:], in_=zT_ps_by_tile[:, 1, 0 : PAIR_RUNS[0][1], :])
+        zT_vector = zT_ps[:].rearrange("s i (a j) -> s i j a", j=N_TILES)
         zT_ps_again = psum_turn.tile([P, ORD, P], BF16, name="turned")
         for i in range(ORD):
             nc.tensor.transpose(
                 out=zT_ps_again[:, i, :], in_=z_rows[:, i, :], identity=ident_bf16[:]
             )
-        zT = keep.tile([P, ORD, N_TILES, R], F32)
-        nc.scalar.copy(out=zT[:], in_=zT_ps_again[:].rearrange("s i (a j) -> s i j a", j=N_TILES))
+        zT_scalar = zT_ps_again[:].rearrange("s i (a j) -> s i j a", j=N_TILES)
 
-        pair_of_tile = {}
-        for first, tiles, on_gpsimd in PAIR_RUNS:
-            run = slice(first, first + tiles)
-            pair = keep.tile([P, tiles, R, R], F32, name="pair%d" % first)
-            if on_gpsimd:
-                nc.gpsimd.tensor_tensor(
-                    out=pair[:],
-                    in0=zT[:, 0, run, :].unsqueeze(2).to_broadcast([P, tiles, R, R]),
-                    in1=zT[:, 1, run, :].unsqueeze(3).to_broadcast([P, tiles, R, R]),
-                    op=MULT,
-                )
-            else:
-                nc.vector.tensor_tensor(
-                    out=pair[:],
-                    in0=zT_ps_by_tile[:, 0, run, :].unsqueeze(2).to_broadcast([P, tiles, R, R]),
-                    in1=z1_first[:].unsqueeze(3).to_broadcast([P, tiles, R, R]),
-                    op=MULT,
-                )
-            for j in range(tiles):
-                pair_of_tile[first + j] = (pair, j)
+        z1_s = keep.tile([P, S_TILES, R], F32)
+        nc.vector.tensor_copy(out=z1_s[:], in_=zT_vector[:, 1, 0:S_TILES, :])
+        pair = keep.tile([P, S_TILES, R, R], F32)
+        nc.vector.tensor_tensor(
+            out=pair[:],
+            in0=zT_vector[:, 0, 0:S_TILES, :].unsqueeze(2).to_broadcast([P, S_TILES, R, R]),
+            in1=z1_s[:].unsqueeze(3).to_broadcast([P, S_TILES, R, R]),
+            op=MULT,
+        )
 
-        def pair_view(g):
-            pair, j = pair_of_tile[FIRST_TILE[g]]
-            return pair[:, j : j + UNIT_TILES[g], :, :].rearrange("s j b a -> s j (b a)")
+        z2_k = keep.tile([P, K_TILES, R], F32)
+        nc.scalar.copy(out=z2_k[:], in_=zT_scalar[:, 2, S_TILES:N_TILES, :])
+        z1_k = keep.tile([P, K_TILES, R, 2], F32)
+        nc.scalar.copy(
+            out=z1_k[:],
+            in_=zT_scalar[:, 1, S_TILES:N_TILES, :].unsqueeze(3).to_broadcast([P, K_TILES, R, 2]),
+        )
+        z2_s = keep.tile([P, S_TILES, R], F32)
+        nc.scalar.copy(out=z2_s[:], in_=zT_scalar[:, 2, 0:S_TILES, :])
+        bank_tiles = BANK // P
+        wT_of_bank = []
+        for bank in range(K_TILES // bank_tiles):
+            tiles = slice(bank * bank_tiles, (bank + 1) * bank_tiles)
+            shape = [P, bank_tiles, R, 2 * R]
+            wT = keep.tile(shape, F32, name="wT%d" % bank)
+            nc.gpsimd.tensor_tensor(
+                out=wT[:],
+                in0=z2_k[:, tiles, :].unsqueeze(3).to_broadcast(shape),
+                in1=z1_k[:, tiles, :, :]
+                .rearrange("s j b d -> s j (b d)")
+                .unsqueeze(2)
+                .to_broadcast(shape),
+                op=MULT,
+            )
+            wT_of_bank.append(wT)
 
         g_words = g_rows[:].bitcast(F32).rearrange("m h (q u) -> m h q u", u=PAIRS)
-        gT_ps = psum_once.tile([P, M_TILES, PAIRS, P], F32)
+        gT_ps = psum_acc.tile([P, M_TILES, PAIRS, P], F32, name="acc")
         for h in range(M_TILES):
             for u in range(PAIRS):
                 nc.tensor.transpose(
@@ -102,71 +128,100 @@ def tile_fast_tucker_taylor_pa_s_kernel(tc, z, G2, out):
         g_scales = keep.tile([P, M], U8, align_bytes=64)
 
         out_by_half = out.rearrange("(h m) n -> m h n", m=P)
+        w_of_bank = {}
         kronT_of = {}
         turned_of = {}
         grouped_of = {}
         codes_of = {}
         acc_of = {}
 
-        def multiply_third_scalar(g):
-            kronT = work.tile([P, UNIT_TILES[g], R, R * R], BF16, name="kronT")
-            kronT_of[g] = kronT
-            for j in range(UNIT_TILES[g]):
-                for c in range(R - SCALAR_C[g], R):
+        def samples_on_partitions(i):
+            return UNITS[i][0] < K_FIRST
+
+        def turn_w(bank):
+            w_ps = psum_once.tile([P, BANK], F32, name="w_ps%d" % bank)
+            for j in range(bank_tiles):
+                nc.tensor.transpose(
+                    out=w_ps[:, j * P : (j + 1) * P],
+                    in_=wT_of_bank[bank][:, j, :, :].rearrange("s c x -> s (c x)"),
+                    identity=ident_f32[:],
+                )
+            w_of_bank[bank] = w_ps
+
+        def multiply_third_scalar(i):
+            first_tile, tiles = UNITS[i][0] // P, UNITS[i][1] // P
+            kronT = work.tile([P, tiles, R, R * R], BF16, name="kronT")
+            kronT_of[i] = kronT
+            for j in range(tiles):
+                for c in range(R - SCALAR_C[i], R):
                     nc.scalar.activation(
                         out=kronT[:, j, c, :],
-                        in_=pair_view(g)[:, j, :],
+                        in_=pair[:, first_tile + j, :, :].rearrange("s b a -> s (b a)"),
                         func=COPY,
-                        scale=zT[:, 2, FIRST_TILE[g] + j, c : c + 1],
+                        scale=z2_s[:, first_tile + j, c : c + 1],
                     )
 
-        def multiply_third_vector(g):
-            tiles = slice(FIRST_TILE[g], FIRST_TILE[g] + UNIT_TILES[g])
-            shape = [P, UNIT_TILES[g], R - SCALAR_C[g], R * R]
+        def multiply_third_vector(i):
+            first_tile, tiles = UNITS[i][0] // P, UNITS[i][1] // P
+            run = slice(first_tile, first_tile + tiles)
+            shape = [P, tiles, R - SCALAR_C[i], R * R]
             nc.vector.tensor_tensor(
-                out=kronT_of[g][:, :, 0 : R - SCALAR_C[g], :],
-                in0=pair_view(g).unsqueeze(2).to_broadcast(shape),
-                in1=zT_ps_by_tile[:, 2, tiles, 0 : R - SCALAR_C[g]].unsqueeze(3).to_broadcast(shape),
+                out=kronT_of[i][:, :, 0 : R - SCALAR_C[i], :],
+                in0=pair[:, run, :, :].rearrange("s j b a -> s j (b a)").unsqueeze(2).to_broadcast(shape),
+                in1=zT_vector[:, 2, run, 0 : R - SCALAR_C[i]].unsqueeze(3).to_broadcast(shape),
                 op=MULT,
             )
 
-        def turn(g):
+        def turn(i):
+            tiles = UNITS[i][1] // P
             words = (
-                kronT_of[g][:]
+                kronT_of[i][:]
                 .rearrange("s j c x -> s j (c x)")
                 .bitcast(F32)
                 .rearrange("s j (q u) -> s j q u", u=PAIRS)
             )
-            turned = psum_turn.tile([P, UNIT_TILES[g], PAIRS, P], F32, name="turned")
-            for j in range(UNIT_TILES[g]):
+            turned = psum_turn.tile([P, tiles, PAIRS, P], F32, name="turned")
+            for j in range(tiles):
                 for u in range(PAIRS):
                     nc.tensor.transpose(
                         out=turned[:, j, u, :], in_=words[:, j, :, u], identity=ident_f32[:]
                     )
-            turned_of[g] = turned
+            turned_of[i] = turned
 
-        def regroup(g):
-            grouped = work.tile([P, UNIT_TILES[g] * P * PACK], BF16, align_bytes=64, name="grouped")
+        def regroup(i):
+            tiles = UNITS[i][1] // P
+            grouped = work.tile([P, UNITS[i][1] * PACK], BF16, align_bytes=64, name="grouped")
             nc.scalar.copy(
-                out=grouped[:]
-                .bitcast(F32)
-                .rearrange("q (j s u) -> q j s u", j=UNIT_TILES[g], u=PAIRS),
-                in_=turned_of[g][:].rearrange("q j u s -> q j s u"),
+                out=grouped[:].bitcast(F32).rearrange("q (j s u) -> q j s u", j=tiles, u=PAIRS),
+                in_=turned_of[i][:].rearrange("q j u s -> q j s u"),
             )
-            grouped_of[g] = grouped
+            grouped_of[i] = grouped
 
-        def quantise(g):
-            k_codes = work.tile([P, UNIT_TILES[g] * P], U32, align_bytes=64, name="k_codes")
-            k_scales = work.tile([P, UNIT_TILES[g] * P], U8, align_bytes=64, name="k_scales")
+        def multiply_spread(i):
+            first, width = UNITS[i][0] - K_FIRST, UNITS[i][1]
+            bank, column = first // BANK, first % BANK
+            grouped = work.tile([P, width * PACK], BF16, align_bytes=64, name="grouped")
+            nc.vector.tensor_tensor(
+                out=grouped[:].rearrange("q (n t) -> q n t", t=PACK),
+                in0=z0_spread[bank][:, :, column : column + width].rearrange("q t n -> q n t"),
+                in1=w_of_bank[bank][:, column : column + width]
+                .unsqueeze(2)
+                .to_broadcast([P, width, PACK]),
+                op=MULT,
+            )
+            grouped_of[i] = grouped
+
+        def quantise(i):
+            k_codes = work.tile([P, UNITS[i][1]], U32, align_bytes=64, name="k_codes")
+            k_scales = work.tile([P, UNITS[i][1]], U8, align_bytes=64, name="k_scales")
             nc.vector.quantize_mx(
-                out=k_codes[:].bitcast(FP8X4), scales=k_scales[:], in_=grouped_of[g][:]
+                out=k_codes[:].bitcast(FP8X4), scales=k_scales[:], in_=grouped_of[i][:]
             )
-            codes_of[g] = (k_codes, k_scales)
+            codes_of[i] = (k_codes, k_scales)
 
-        def product(g):
-            k_codes, k_scales = codes_of[g]
-            width = UNIT_TILES[g] * P
-            acc = psum_acc.tile([P, M_TILES, width], F32, name="acc")
+        def product(i):
+            k_codes, k_scales = codes_of[i]
+            acc = psum_acc.tile([P, M_TILES, UNITS[i][1]], F32, name="acc")
             for h in range(M_TILES):
                 rows = slice(h * P, (h + 1) * P)
                 nc.tensor.matmul_mx(
@@ -178,21 +233,22 @@ def tile_fast_tucker_taylor_pa_s_kernel(tc, z, G2, out):
                     start=True,
                     stop=True,
                 )
-            acc_of[g] = acc
+            acc_of[i] = acc
 
-        def store(g):
-            width = UNIT_TILES[g] * P
+        def store(i):
+            first, width = UNITS[i]
             result = work.tile([P, M_TILES, width], F32, name="result")
-            if g in VECTOR_RESULTS:
-                nc.vector.tensor_copy(out=result[:], in_=acc_of[g][:])
+            if i in VECTOR_RESULTS:
+                nc.vector.tensor_copy(out=result[:], in_=acc_of[i][:])
             else:
-                nc.scalar.copy(out=result[:], in_=acc_of[g][:])
-            first = FIRST_TILE[g] * P
+                nc.scalar.copy(out=result[:], in_=acc_of[i][:])
             nc.sync.dma_start(out=out_by_half[:, :, first : first + width], in_=result[:])
 
-        for step in range(UNITS + 4):
-            if step < UNITS:
-                multiply_third_scalar(step)
+        count = len(UNITS)
+        quantise_step = [
+            max(i + (3 if samples_on_partitions(i) else 2), FIRST_QUANTISE) for i in range(count)
+        ]
+        for step in range(max(quantise_step) + 2):
             if step == 1:
                 nc.scalar.copy(
                     out=g_grouped[:]
@@ -200,20 +256,31 @@ def tile_fast_tucker_taylor_pa_s_kernel(tc, z, G2, out):
                     .rearrange("q (h m u) -> q h m u", h=M_TILES, u=PAIRS),
                     in_=gT_ps[:].rearrange("q h u m -> q h m u"),
                 )
-            if 0 <= step - 2 < UNITS:
+            if 0 <= step - 2 < count and samples_on_partitions(step - 2):
                 regroup(step - 2)
-            if 0 <= step - 4 < UNITS:
-                product(step - 4)
-                if step - 4 not in VECTOR_RESULTS:
-                    store(step - 4)
-            if 0 <= step - 1 < UNITS:
-                multiply_third_vector(step - 1)
-                turn(step - 1)
-            if step == 3:
+            for i in range(count):
+                if quantise_step[i] + 1 == step:
+                    product(i)
+                    if i not in VECTOR_RESULTS:
+                        store(i)
+            for i in range(count):
+                if samples_on_partitions(i) and SCALAR_STEP[i] == step:
+                    multiply_third_scalar(i)
+            if step in TURN_W_STEP:
+                turn_w(TURN_W_STEP.index(step))
+            if 0 <= step - 1 < count:
+                if samples_on_partitions(step - 1):
+                    multiply_third_vector(step - 1)
+                    turn(step - 1)
+                else:
+                    multiply_spread(step - 1)
+            if step == FIRST_QUANTISE:
                 nc.vector.quantize_mx(
                     out=g_codes[:].bitcast(FP8X4), scales=g_scales[:], in_=g_grouped[:]
                 )
-            if 0 <= step - 3 < UNITS:
-                quantise(step - 3)
-            if step - 4 in VECTOR_RESULTS:
-                store(step - 4)
+            for i in range(count):
+                if quantise_step[i] == step:
+                    quantise(i)
+            for i in VECTOR_RESULTS:
+                if quantise_step[i] + 1 == step:
+                    store(i)

@@ -49,6 +49,7 @@ def tile_fast_tucker_taylor_pa_s_kernel(tc, z, G2, out):
         z_rows = keep.tile([P, ORD, P], BF16)
         nc.sync.dma_start(out=z_rows[:], in_=z.rearrange("i a (j s) -> (a j) i s", s=P))
         g_rows = keep.tile([P, M_TILES, K], BF16)
+        nc.sync.dma_start(out=g_rows[:], in_=G2.rearrange("(h m) k -> m h k", m=P))
         z0_spread = []
         for bank in range(K_TILES * P // BANK):
             spread = keep.tile([P, PACK, BANK], BF16, name="z0_spread%d" % bank)
@@ -61,8 +62,6 @@ def tile_fast_tucker_taylor_pa_s_kernel(tc, z, G2, out):
                     .to_broadcast([P // 2, PACK, BANK]),
                 )
             z0_spread.append(spread)
-            if bank == 0:
-                nc.sync.dma_start(out=g_rows[:], in_=G2.rearrange("(h m) k -> m h k", m=P))
 
         ident_bf16 = keep.tile([P, P], BF16)
         make_identity(nc, ident_bf16[:])

@@ -27,7 +27,7 @@ S_TILES = 8
 K_TILES = N_TILES - S_TILES
 K_FIRST = S_TILES * P
 UNITS = ((0, 256), (256, 256), (512, 256), (1024, 256), (1280, 256), (768, 256), (1536, 256), (1792, 128), (1920, 128))
-SCALAR_C = (2, 2, 2, 0, 0, 6, 0, 0, 0)
+SCALAR_C = (2, 2, 2, 0, 0, 4, 0, 0, 0)
 SCALAR_STEP = (0, 0, 1, 0, 0, 4, 0, 0, 0)
 FIRST_QUANTISE = 4
 VECTOR_RESULTS = (8,)

@@ -13,6 +13,7 @@ COPY = mybir.ActivationFunctionType.Copy
 
 P = 128
 ORD = 3
+FACTOR_ORDER = (1, 0, 2)
 R = 8
 K = R**ORD
 PACK = 4
@@ -32,6 +33,7 @@ SCALAR_STEP = (0, 0, 1, 0, 0, 4, 0, 0, 0)
 FIRST_QUANTISE = 4
 VECTOR_RESULTS = (8,)
 TURN_W_STEP = (2, 4)
+PAIR_RUNS = (slice(0, 2), slice(2, S_TILES))
 
 FLOPS = 2 * M * K * N
 
@@ -47,7 +49,8 @@ def tile_fast_tucker_taylor_pa_s_kernel(tc, z, G2, out):
         ctx.enter_context(tc.manual_schedule())
 
         z_rows = keep.tile([P, ORD, P], BF16)
-        nc.sync.dma_start(out=z_rows[:], in_=z.rearrange("i a (j s) -> (a j) i s", s=P))
+        for i in FACTOR_ORDER:
+            nc.sync.dma_start(out=z_rows[:, i, :], in_=z[i].rearrange("a (j s) -> (a j) s", s=P))
         g_rows = keep.tile([P, M_TILES, K], BF16)
         nc.sync.dma_start(out=g_rows[:], in_=G2.rearrange("(h m) k -> m h k", m=P))
         z0_spread = []
@@ -68,36 +71,34 @@ def tile_fast_tucker_taylor_pa_s_kernel(tc, z, G2, out):
         ident_f32 = keep.tile([P, P], F32)
         make_identity(nc, ident_f32[:])
 
-        zT_ps = psum_once.tile([P, ORD, P], BF16)
-        for i in range(ORD):
-            nc.tensor.transpose(out=zT_ps[:, i, :], in_=z_rows[:, i, :], identity=ident_bf16[:])
-        zT_vector = zT_ps[:].rearrange("s i (a j) -> s i j a", j=N_TILES)
-        zT_ps_again = psum_turn.tile([P, ORD, P], BF16, name="turned")
-        for i in range(ORD):
-            nc.tensor.transpose(
-                out=zT_ps_again[:, i, :], in_=z_rows[:, i, :], identity=ident_bf16[:]
-            )
-        zT_scalar = zT_ps_again[:].rearrange("s i (a j) -> s i j a", j=N_TILES)
+        zT = {}
+        for i in FACTOR_ORDER:
+            pool = psum_once if i == 2 else psum_acc
+            zT_ps = pool.tile([P, P], BF16, name="zT2" if i == 2 else "acc")
+            nc.tensor.transpose(out=zT_ps[:], in_=z_rows[:, i, :], identity=ident_bf16[:])
+            zT[i] = zT_ps[:].rearrange("s (a j) -> s j a", j=N_TILES)
 
         z1_s = keep.tile([P, S_TILES, R], F32)
-        nc.vector.tensor_copy(out=z1_s[:], in_=zT_vector[:, 1, 0:S_TILES, :])
+        nc.vector.tensor_copy(out=z1_s[:], in_=zT[1][:, 0:S_TILES, :])
         pair = keep.tile([P, S_TILES, R, R], F32)
-        nc.vector.tensor_tensor(
-            out=pair[:],
-            in0=zT_vector[:, 0, 0:S_TILES, :].unsqueeze(2).to_broadcast([P, S_TILES, R, R]),
-            in1=z1_s[:].unsqueeze(3).to_broadcast([P, S_TILES, R, R]),
-            op=MULT,
-        )
+        for run in PAIR_RUNS:
+            shape = [P, run.stop - run.start, R, R]
+            nc.vector.tensor_tensor(
+                out=pair[:, run, :, :],
+                in0=zT[0][:, run, :].unsqueeze(2).to_broadcast(shape),
+                in1=z1_s[:, run, :].unsqueeze(3).to_broadcast(shape),
+                op=MULT,
+            )
 
-        z2_k = keep.tile([P, K_TILES, R], F32)
-        nc.scalar.copy(out=z2_k[:], in_=zT_scalar[:, 2, S_TILES:N_TILES, :])
         z1_k = keep.tile([P, K_TILES, R, 2], F32)
         nc.scalar.copy(
             out=z1_k[:],
-            in_=zT_scalar[:, 1, S_TILES:N_TILES, :].unsqueeze(3).to_broadcast([P, K_TILES, R, 2]),
+            in_=zT[1][:, S_TILES:N_TILES, :].unsqueeze(3).to_broadcast([P, K_TILES, R, 2]),
         )
+        z2_k = keep.tile([P, K_TILES, R], F32)
+        nc.scalar.copy(out=z2_k[:], in_=zT[2][:, S_TILES:N_TILES, :])
         z2_s = keep.tile([P, S_TILES, R], F32)
-        nc.scalar.copy(out=z2_s[:], in_=zT_scalar[:, 2, 0:S_TILES, :])
+        nc.scalar.copy(out=z2_s[:], in_=zT[2][:, 0:S_TILES, :])
         bank_tiles = BANK // P
         wT_of_bank = []
         for bank in range(K_TILES // bank_tiles):
@@ -167,7 +168,7 @@ def tile_fast_tucker_taylor_pa_s_kernel(tc, z, G2, out):
             nc.vector.tensor_tensor(
                 out=kronT_of[i][:, :, 0 : R - SCALAR_C[i], :],
                 in0=pair[:, run, :, :].rearrange("s j b a -> s j (b a)").unsqueeze(2).to_broadcast(shape),
-                in1=zT_vector[:, 2, run, 0 : R - SCALAR_C[i]].unsqueeze(3).to_broadcast(shape),
+                in1=zT[2][:, run, 0 : R - SCALAR_C[i]].unsqueeze(3).to_broadcast(shape),
                 op=MULT,
             )
 

@@ -27,13 +27,20 @@ BANK = 512
 S_TILES = 8
 K_TILES = N_TILES - S_TILES
 K_FIRST = S_TILES * P
-UNITS = ((0, 256), (256, 256), (512, 256), (1024, 256), (1280, 256), (768, 256), (1536, 256), (1792, 128), (1920, 128))
-SCALAR_C = (2, 2, 2, 0, 0, 4, 0, 0, 0)
-SCALAR_STEP = (0, 0, 1, 0, 0, 4, 0, 0, 0)
-FIRST_QUANTISE = 4
-VECTOR_RESULTS = (8,)
-TURN_W_STEP = (2, 4)
-PAIR_RUNS = (slice(0, 2), slice(2, S_TILES))
+UNITS = {
+    "n0": (0, 256),
+    "n1": (256, 256),
+    "n2": (512, 256),
+    "g": (768, 256),
+    "k0": (1024, 256),
+    "k1": (1280, 256),
+    "k2": (1536, 256),
+    "k3": (1792, 128),
+    "k4": (1920, 128),
+}
+PAIR_RUNS = (slice(0, 2), slice(2, 8))
+GATE = "n1"
+LAST = "k4"
 
 FLOPS = 2 * M * K * N
 
@@ -45,6 +52,7 @@ def tile_fast_tucker_taylor_pa_s_kernel(tc, z, G2, out):
         work = ctx.enter_context(tc.tile_pool(name="work", bufs=5))
         psum_once = ctx.enter_context(tc.psum_pool(name="psum_once", bufs=1))
         psum_turn = ctx.enter_context(tc.psum_pool(name="psum_turn", bufs=2))
+        psum_w = ctx.enter_context(tc.psum_pool(name="psum_w", bufs=2))
         psum_acc = ctx.enter_context(tc.psum_pool(name="psum_acc", bufs=3))
         ctx.enter_context(tc.manual_schedule())
 
@@ -99,23 +107,6 @@ def tile_fast_tucker_taylor_pa_s_kernel(tc, z, G2, out):
         nc.scalar.copy(out=z2_k[:], in_=zT[2][:, S_TILES:N_TILES, :])
         z2_s = keep.tile([P, S_TILES, R], F32)
         nc.scalar.copy(out=z2_s[:], in_=zT[2][:, 0:S_TILES, :])
-        bank_tiles = BANK // P
-        wT_of_bank = []
-        for bank in range(K_TILES // bank_tiles):
-            tiles = slice(bank * bank_tiles, (bank + 1) * bank_tiles)
-            shape = [P, bank_tiles, R, 2 * R]
-            wT = keep.tile(shape, F32, name="wT%d" % bank)
-            nc.gpsimd.tensor_tensor(
-                out=wT[:],
-                in0=z2_k[:, tiles, :].unsqueeze(3).to_broadcast(shape),
-                in1=z1_k[:, tiles, :, :]
-                .rearrange("s j b d -> s j (b d)")
-                .unsqueeze(2)
-                .to_broadcast(shape),
-                op=MULT,
-            )
-            wT_of_bank.append(wT)
-
         g_words = g_rows[:].bitcast(F32).rearrange("m h (q u) -> m h q u", u=PAIRS)
         gT_ps = psum_acc.tile([P, M_TILES, PAIRS, P], F32, name="acc")
         for h in range(M_TILES):
@@ -135,93 +126,129 @@ def tile_fast_tucker_taylor_pa_s_kernel(tc, z, G2, out):
         codes_of = {}
         acc_of = {}
 
-        def samples_on_partitions(i):
-            return UNITS[i][0] < K_FIRST
+        wT_of = {}
+        bank_tiles = BANK // P
+
+        def multiply_w(bank):
+            run = slice(bank * bank_tiles, (bank + 1) * bank_tiles)
+            shape = [P, bank_tiles, R, 2 * R]
+            wT = keep.tile(shape, F32, name="wT%d" % bank)
+            nc.gpsimd.tensor_tensor(
+                out=wT[:],
+                in0=z2_k[:, run, :].unsqueeze(3).to_broadcast(shape),
+                in1=z1_k[:, run, :, :].rearrange("s j b d -> s j (b d)").unsqueeze(2).to_broadcast(shape),
+                op=MULT,
+            )
+            wT_of[bank] = wT
 
         def turn_w(bank):
-            w_ps = psum_once.tile([P, BANK], F32, name="w_ps%d" % bank)
+            w_ps = psum_w.tile([P, BANK], F32, name="w_ps")
             for j in range(bank_tiles):
                 nc.tensor.transpose(
                     out=w_ps[:, j * P : (j + 1) * P],
-                    in_=wT_of_bank[bank][:, j, :, :].rearrange("s c x -> s (c x)"),
+                    in_=wT_of[bank][:, j, :, :].rearrange("s c x -> s (c x)"),
                     identity=ident_f32[:],
                 )
             w_of_bank[bank] = w_ps
 
-        def multiply_third_scalar(i):
-            first_tile, tiles = UNITS[i][0] // P, UNITS[i][1] // P
+        def samples_unit(u):
+            tiles = UNITS[u][1] // P
             kronT = work.tile([P, tiles, R, R * R], BF16, name="kronT")
-            kronT_of[i] = kronT
-            for j in range(tiles):
-                for c in range(R - SCALAR_C[i], R):
-                    nc.scalar.activation(
-                        out=kronT[:, j, c, :],
-                        in_=pair[:, first_tile + j, :, :].rearrange("s b a -> s (b a)"),
-                        func=COPY,
-                        scale=z2_s[:, first_tile + j, c : c + 1],
-                    )
+            kronT_of[u] = kronT
 
-        def multiply_third_vector(i):
-            first_tile, tiles = UNITS[i][0] // P, UNITS[i][1] // P
+        def gpsimd_tile(u, tile, gate):
+            kronT = keep.tile([P, 1, R, R * R], BF16, align_bytes=64, name="gate" if gate else "kronT_%s%d" % (u, tile))
+            kronT_of.setdefault(u, {})[tile] = kronT
+
+        def multiply_scalar(u, tile, first_c):
+            j = UNITS[u][0] // P + tile
+            for c in range(first_c, R):
+                nc.scalar.activation(
+                    out=kronT_of[u][:, tile, c, :],
+                    in_=pair[:, j, :, :].rearrange("s b a -> s (b a)"),
+                    func=COPY,
+                    scale=z2_s[:, j, c : c + 1],
+                )
+
+        def multiply_vector(u, last_c=R):
+            first_tile, tiles = UNITS[u][0] // P, UNITS[u][1] // P
             run = slice(first_tile, first_tile + tiles)
-            shape = [P, tiles, R - SCALAR_C[i], R * R]
+            shape = [P, tiles, last_c, R * R]
             nc.vector.tensor_tensor(
-                out=kronT_of[i][:, :, 0 : R - SCALAR_C[i], :],
+                out=kronT_of[u][:, :, 0:last_c, :],
                 in0=pair[:, run, :, :].rearrange("s j b a -> s j (b a)").unsqueeze(2).to_broadcast(shape),
-                in1=zT[2][:, run, 0 : R - SCALAR_C[i]].unsqueeze(3).to_broadcast(shape),
+                in1=zT[2][:, run, 0:last_c].unsqueeze(3).to_broadcast(shape),
                 op=MULT,
             )
 
-        def turn(i):
-            tiles = UNITS[i][1] // P
-            words = (
-                kronT_of[i][:]
-                .rearrange("s j c x -> s j (c x)")
-                .bitcast(F32)
-                .rearrange("s j (q u) -> s j q u", u=PAIRS)
+        def multiply_vector_tile(u, tile, last_c):
+            first_tile = UNITS[u][0] // P + tile
+            run = slice(first_tile, first_tile + 1)
+            shape = [P, 1, last_c, R * R]
+            nc.vector.tensor_tensor(
+                out=kronT_of[u][:, tile : tile + 1, 0:last_c, :],
+                in0=pair[:, run, :, :].rearrange("s j b a -> s j (b a)").unsqueeze(2).to_broadcast(shape),
+                in1=zT[2][:, run, 0:last_c].unsqueeze(3).to_broadcast(shape),
+                op=MULT,
             )
+
+        def multiply_gpsimd(u, tile):
+            first_tile = UNITS[u][0] // P + tile
+            run = slice(first_tile, first_tile + 1)
+            shape = [P, 1, R, R * R]
+            nc.gpsimd.tensor_tensor(
+                out=kronT_of[u][tile][:, 0:1, :, :],
+                in0=pair[:, run, :, :].rearrange("s j b a -> s j (b a)").unsqueeze(2).to_broadcast(shape),
+                in1=z2_s[:, run, :].unsqueeze(3).to_broadcast(shape),
+                op=MULT,
+            )
+
+        def turn(u):
+            tiles = UNITS[u][1] // P
             turned = psum_turn.tile([P, tiles, PAIRS, P], F32, name="turned")
             for j in range(tiles):
-                for u in range(PAIRS):
+                kronT = kronT_of[u][j][:, 0, :, :] if isinstance(kronT_of[u], dict) else kronT_of[u][:, j, :, :]
+                words = kronT.rearrange("s c x -> s (c x)").bitcast(F32).rearrange("s (q u) -> s q u", u=PAIRS)
+                for half in range(PAIRS):
                     nc.tensor.transpose(
-                        out=turned[:, j, u, :], in_=words[:, j, :, u], identity=ident_f32[:]
+                        out=turned[:, j, half, :], in_=words[:, :, half], identity=ident_f32[:]
                     )
-            turned_of[i] = turned
+            turned_of[u] = turned
 
-        def regroup(i):
-            tiles = UNITS[i][1] // P
-            grouped = work.tile([P, UNITS[i][1] * PACK], BF16, align_bytes=64, name="grouped")
+        def regroup(u):
+            tiles = UNITS[u][1] // P
+            pool, name = (keep, "gate") if u == GATE else (work, "grouped")
+            grouped = pool.tile([P, UNITS[u][1] * PACK], BF16, align_bytes=64, name=name)
             nc.scalar.copy(
                 out=grouped[:].bitcast(F32).rearrange("q (j s u) -> q j s u", j=tiles, u=PAIRS),
-                in_=turned_of[i][:].rearrange("q j u s -> q j s u"),
+                in_=turned_of[u][:].rearrange("q j u s -> q j s u"),
             )
-            grouped_of[i] = grouped
+            grouped_of[u] = grouped
 
-        def multiply_spread(i):
-            first, width = UNITS[i][0] - K_FIRST, UNITS[i][1]
+        def multiply_spread(u):
+            first, width = UNITS[u][0] - K_FIRST, UNITS[u][1]
             bank, column = first // BANK, first % BANK
             grouped = work.tile([P, width * PACK], BF16, align_bytes=64, name="grouped")
             nc.vector.tensor_tensor(
                 out=grouped[:].rearrange("q (n t) -> q n t", t=PACK),
                 in0=z0_spread[bank][:, :, column : column + width].rearrange("q t n -> q n t"),
-                in1=w_of_bank[bank][:, column : column + width]
-                .unsqueeze(2)
-                .to_broadcast([P, width, PACK]),
+                in1=w_of_bank[bank][:, column : column + width].unsqueeze(2).to_broadcast([P, width, PACK]),
                 op=MULT,
             )
-            grouped_of[i] = grouped
+            grouped_of[u] = grouped
 
-        def quantise(i):
-            k_codes = work.tile([P, UNITS[i][1]], U32, align_bytes=64, name="k_codes")
-            k_scales = work.tile([P, UNITS[i][1]], U8, align_bytes=64, name="k_scales")
+        def quantise(u):
+            k_codes = work.tile([P, UNITS[u][1]], U32, align_bytes=64, name="k_codes")
+            k_scales = work.tile([P, UNITS[u][1]], U8, align_bytes=64, name="k_scales")
             nc.vector.quantize_mx(
-                out=k_codes[:].bitcast(FP8X4), scales=k_scales[:], in_=grouped_of[i][:]
+                out=k_codes[:].bitcast(FP8X4), scales=k_scales[:], in_=grouped_of[u][:]
             )
-            codes_of[i] = (k_codes, k_scales)
+            codes_of[u] = (k_codes, k_scales)
 
-        def product(i):
-            k_codes, k_scales = codes_of[i]
-            acc = psum_acc.tile([P, M_TILES, UNITS[i][1]], F32, name="acc")
+        def product(u):
+            k_codes, k_scales = codes_of[u]
+            pool, name = (psum_w, "w_ps") if u == LAST else (psum_acc, "acc")
+            acc = pool.tile([P, M_TILES, UNITS[u][1]], F32, name=name)
             for h in range(M_TILES):
                 rows = slice(h * P, (h + 1) * P)
                 nc.tensor.matmul_mx(
@@ -233,54 +260,87 @@ def tile_fast_tucker_taylor_pa_s_kernel(tc, z, G2, out):
                     start=True,
                     stop=True,
                 )
-            acc_of[i] = acc
+            acc_of[u] = acc
 
-        def store(i):
-            first, width = UNITS[i]
-            result = work.tile([P, M_TILES, width], F32, name="result")
-            if i in VECTOR_RESULTS:
-                nc.vector.tensor_copy(out=result[:], in_=acc_of[i][:])
+        def store(u, engine):
+            first, width = UNITS[u]
+            result = keep.tile([P, M_TILES, width], F32, name="result_" + u)
+            if engine == "vector":
+                nc.vector.tensor_copy(out=result[:], in_=acc_of[u][:])
             else:
-                nc.scalar.copy(out=result[:], in_=acc_of[i][:])
+                nc.scalar.copy(out=result[:], in_=acc_of[u][:])
             nc.sync.dma_start(out=out_by_half[:, :, first : first + width], in_=result[:])
 
-        count = len(UNITS)
-        quantise_step = [
-            max(i + (3 if samples_on_partitions(i) else 2), FIRST_QUANTISE) for i in range(count)
-        ]
-        for step in range(max(quantise_step) + 2):
-            if step == 1:
-                nc.scalar.copy(
-                    out=g_grouped[:]
-                    .bitcast(F32)
-                    .rearrange("q (h m u) -> q h m u", h=M_TILES, u=PAIRS),
-                    in_=gT_ps[:].rearrange("q h u m -> q h m u"),
-                )
-            if 0 <= step - 2 < count and samples_on_partitions(step - 2):
-                regroup(step - 2)
-            for i in range(count):
-                if quantise_step[i] + 1 == step:
-                    product(i)
-                    if i not in VECTOR_RESULTS:
-                        store(i)
-            for i in range(count):
-                if samples_on_partitions(i) and SCALAR_STEP[i] == step:
-                    multiply_third_scalar(i)
-            if step in TURN_W_STEP:
-                turn_w(TURN_W_STEP.index(step))
-            if 0 <= step - 1 < count:
-                if samples_on_partitions(step - 1):
-                    multiply_third_vector(step - 1)
-                    turn(step - 1)
-                else:
-                    multiply_spread(step - 1)
-            if step == FIRST_QUANTISE:
-                nc.vector.quantize_mx(
-                    out=g_codes[:].bitcast(FP8X4), scales=g_scales[:], in_=g_grouped[:]
-                )
-            for i in range(count):
-                if quantise_step[i] == step:
-                    quantise(i)
-            for i in VECTOR_RESULTS:
-                if quantise_step[i] + 1 == step:
-                    store(i)
+        def quantise_g():
+            nc.vector.quantize_mx(
+                out=g_codes[:].bitcast(FP8X4), scales=g_scales[:], in_=g_grouped[:]
+            )
+
+        def regroup_g():
+            nc.scalar.copy(
+                out=g_grouped[:].bitcast(F32).rearrange("q (h m u) -> q h m u", h=M_TILES, u=PAIRS),
+                in_=gT_ps[:].rearrange("q h u m -> q h m u"),
+            )
+
+        samples_unit("n0")
+        samples_unit("n1")
+        samples_unit("n2")
+        gpsimd_tile("g", 0, False)
+        multiply_w(0)
+        multiply_w(1)
+        multiply_gpsimd("g", 0)
+        multiply_scalar("n0", 0, 5)
+        multiply_scalar("n0", 1, 5)
+        multiply_vector("n0", 5)
+        regroup_g()
+        turn("n0")
+        multiply_scalar("n1", 0, 5)
+        multiply_scalar("n1", 1, 5)
+        multiply_vector("n1", 5)
+        turn_w(0)
+        multiply_scalar("n2", 0, 5)
+        multiply_scalar("n2", 1, 5)
+        regroup("n0")
+        turn("n1")
+        multiply_vector("n2", 5)
+        regroup("n1")
+        turn("n2")
+        multiply_spread("k0")
+        turn_w(1)
+        regroup("n2")
+        quantise_g()
+        quantise("n0")
+        product("n0")
+        store("n0", "scalar")
+        quantise("n1")
+        product("n1")
+        gpsimd_tile("g", 1, True)
+        multiply_gpsimd("g", 1)
+        store("n1", "scalar")
+        multiply_spread("k1")
+        quantise("k0")
+        product("k0")
+        turn("g")
+        store("k0", "scalar")
+        quantise("n2")
+        product("n2")
+        regroup("g")
+        store("n2", "scalar")
+        quantise("k1")
+        product("k1")
+        multiply_spread("k2")
+        store("k1", "scalar")
+        multiply_spread("k3")
+        quantise("g")
+        product("g")
+        store("g", "scalar")
+        quantise("k2")
+        product("k2")
+        store("k2", "scalar")
+        multiply_spread("k4")
+        quantise("k3")
+        product("k3")
+        store("k3", "scalar")
+        quantise("k4")
+        product("k4")
+        store("k4", "vector")

@@ -79,24 +79,36 @@ def tile_fast_tucker_taylor_pa_s_kernel(tc, z, G2, out):
         ident_f32 = keep.tile([P, P], F32)
         make_identity(nc, ident_f32[:])
 
+        ident_order = keep.tile([P, N_TILES, PAIRS, 2, 2], BF16)
+        for u in range(PAIRS):
+            nc.vector.tensor_copy(
+                out=ident_order[:, :, u, :, :],
+                in_=ident_bf16[:].rearrange("p (d u e j) -> p u j d e", d=2, u=PAIRS, e=2)[:, u, :, :, :],
+            )
+
         zT = {}
         for i in FACTOR_ORDER:
             pool = psum_once if i == 2 else psum_acc
             zT_ps = pool.tile([P, P], BF16, name="zT2" if i == 2 else "acc")
-            nc.tensor.transpose(out=zT_ps[:], in_=z_rows[:, i, :], identity=ident_bf16[:])
-            zT[i] = zT_ps[:].rearrange("s (a j) -> s j a", j=N_TILES)
+            order = ident_order[:].rearrange("p j u d e -> p (j u d e)") if i == 0 else ident_bf16[:]
+            nc.tensor.transpose(out=zT_ps[:], in_=z_rows[:, i, :], identity=order)
+            zT[i] = zT_ps[:] if i == 0 else zT_ps[:].rearrange("s (a j) -> s j a", j=N_TILES)
 
-        z1_s = keep.tile([P, S_TILES, R], F32)
-        nc.vector.tensor_copy(out=z1_s[:], in_=zT[1][:, 0:S_TILES, :])
-        pair = keep.tile([P, S_TILES, R, R], F32)
+        z1_s = keep.tile([P, S_TILES, PAIRS, R], F32)
+        nc.vector.tensor_copy(
+            out=z1_s[:], in_=zT[1][:, 0:S_TILES, :].unsqueeze(2).to_broadcast([P, S_TILES, PAIRS, R])
+        )
+        pair = keep.tile([P, S_TILES * PAIRS, R, 4], F32)
         for run in PAIR_RUNS:
-            shape = [P, run.stop - run.start, R, R]
+            halves = slice(run.start * PAIRS, run.stop * PAIRS)
+            shape = [P, halves.stop - halves.start, R, 4]
             nc.vector.tensor_tensor(
-                out=pair[:, run, :, :],
-                in0=zT[0][:, run, :].unsqueeze(2).to_broadcast(shape),
-                in1=z1_s[:, run, :].unsqueeze(3).to_broadcast(shape),
+                out=pair[:, halves, :, :],
+                in0=zT[0].rearrange("s (h x) -> s h x", x=4)[:, halves, :].unsqueeze(2).to_broadcast(shape),
+                in1=z1_s[:].rearrange("s j u b -> s (j u) b")[:, halves, :].unsqueeze(3).to_broadcast(shape),
                 op=MULT,
             )
+        pair = pair[:].rearrange("s (j u) b x -> s j u (b x)", u=PAIRS)
 
         z1_k = keep.tile([P, K_TILES, R, 2], F32)
         nc.scalar.copy(
@@ -153,53 +165,42 @@ def tile_fast_tucker_taylor_pa_s_kernel(tc, z, G2, out):
 
         def samples_unit(u):
             tiles = UNITS[u][1] // P
-            kronT = work.tile([P, tiles, R, R * R], BF16, name="kronT")
+            kronT = work.tile([P, tiles, PAIRS, R, R * R // PAIRS], BF16, name="kronT")
             kronT_of[u] = kronT
 
         def gpsimd_tile(u, tile, gate):
-            kronT = keep.tile([P, 1, R, R * R], BF16, align_bytes=64, name="gate" if gate else "kronT_%s%d" % (u, tile))
+            kronT = keep.tile([P, 1, PAIRS, R, R * R // PAIRS], BF16, align_bytes=64, name="gate" if gate else "kronT_%s%d" % (u, tile))
             kronT_of.setdefault(u, {})[tile] = kronT
 
         def multiply_scalar(u, tile, first_c):
             j = UNITS[u][0] // P + tile
             for c in range(first_c, R):
                 nc.scalar.activation(
-                    out=kronT_of[u][:, tile, c, :],
-                    in_=pair[:, j, :, :].rearrange("s b a -> s (b a)"),
+                    out=kronT_of[u][:, tile, :, c, :],
+                    in_=pair[:, j, :, :],
                     func=COPY,
                     scale=z2_s[:, j, c : c + 1],
                 )
 
         def multiply_vector(u, last_c=R):
             first_tile, tiles = UNITS[u][0] // P, UNITS[u][1] // P
-            run = slice(first_tile, first_tile + tiles)
-            shape = [P, tiles, last_c, R * R]
-            nc.vector.tensor_tensor(
-                out=kronT_of[u][:, :, 0:last_c, :],
-                in0=pair[:, run, :, :].rearrange("s j b a -> s j (b a)").unsqueeze(2).to_broadcast(shape),
-                in1=zT[2][:, run, 0:last_c].unsqueeze(3).to_broadcast(shape),
-                op=MULT,
-            )
-
-        def multiply_vector_tile(u, tile, last_c):
-            first_tile = UNITS[u][0] // P + tile
-            run = slice(first_tile, first_tile + 1)
-            shape = [P, 1, last_c, R * R]
-            nc.vector.tensor_tensor(
-                out=kronT_of[u][:, tile : tile + 1, 0:last_c, :],
-                in0=pair[:, run, :, :].rearrange("s j b a -> s j (b a)").unsqueeze(2).to_broadcast(shape),
-                in1=zT[2][:, run, 0:last_c].unsqueeze(3).to_broadcast(shape),
-                op=MULT,
-            )
+            shape = [P, PAIRS, last_c, R * R // PAIRS]
+            for tile in range(tiles):
+                nc.vector.tensor_tensor(
+                    out=kronT_of[u][:, tile, :, 0:last_c, :],
+                    in0=pair[:, first_tile + tile, :, :].unsqueeze(2).to_broadcast(shape),
+                    in1=zT[2][:, first_tile + tile, 0:last_c].unsqueeze(1).unsqueeze(3).to_broadcast(shape),
+                    op=MULT,
+                )
 
         def multiply_gpsimd(u, tile):
             first_tile = UNITS[u][0] // P + tile
             run = slice(first_tile, first_tile + 1)
-            shape = [P, 1, R, R * R]
+            shape = [P, PAIRS, R, R * R // PAIRS]
             nc.gpsimd.tensor_tensor(
-                out=kronT_of[u][tile][:, 0:1, :, :],
-                in0=pair[:, run, :, :].rearrange("s j b a -> s j (b a)").unsqueeze(2).to_broadcast(shape),
-                in1=z2_s[:, run, :].unsqueeze(3).to_broadcast(shape),
+                out=kronT_of[u][tile][:, 0, :, :, :],
+                in0=pair[:, first_tile, :, :].unsqueeze(2).to_broadcast(shape),
+                in1=z2_s[:, first_tile, :].unsqueeze(1).unsqueeze(3).to_broadcast(shape),
                 op=MULT,
             )
 
@@ -207,11 +208,11 @@ def tile_fast_tucker_taylor_pa_s_kernel(tc, z, G2, out):
             tiles = UNITS[u][1] // P
             turned = psum_turn.tile([P, tiles, PAIRS, P], F32, name="turned")
             for j in range(tiles):
-                kronT = kronT_of[u][j][:, 0, :, :] if isinstance(kronT_of[u], dict) else kronT_of[u][:, j, :, :]
-                words = kronT.rearrange("s c x -> s (c x)").bitcast(F32).rearrange("s (q u) -> s q u", u=PAIRS)
+                kronT = kronT_of[u][j][:, 0] if isinstance(kronT_of[u], dict) else kronT_of[u][:, j]
+                words = kronT.rearrange("s u c x -> s (u c x)").bitcast(F32).rearrange("s (u q) -> s u q", u=PAIRS)
                 for half in range(PAIRS):
                     nc.tensor.transpose(
-                        out=turned[:, j, half, :], in_=words[:, :, half], identity=ident_f32[:]
+                        out=turned[:, j, half, :], in_=words[:, half, :], identity=ident_f32[:]
                     )
             turned_of[u] = turned
 

@@ -39,7 +39,7 @@ UNITS = {
     "k4": (1920, 128),
 }
 PAIR_RUNS = (slice(0, 2), slice(2, 8))
-GATE = "n1"
+GATES = {"n1": "gate"}
 LAST = "k4"
 
 FLOPS = 2 * M * K * N
@@ -163,44 +163,33 @@ def tile_fast_tucker_taylor_pa_s_kernel(tc, z, G2, out):
                 )
             w_of_bank[bank] = w_ps
 
-        def samples_unit(u):
-            tiles = UNITS[u][1] // P
-            kronT = work.tile([P, tiles, PAIRS, R, R * R // PAIRS], BF16, name="kronT")
-            kronT_of[u] = kronT
+        def new_kronT(j, pool, name):
+            kronT_of[j] = pool.tile([P, PAIRS, R, R * R // PAIRS], BF16, align_bytes=64, name=name)
 
-        def gpsimd_tile(u, tile, gate):
-            kronT = keep.tile([P, 1, PAIRS, R, R * R // PAIRS], BF16, align_bytes=64, name="gate" if gate else "kronT_%s%d" % (u, tile))
-            kronT_of.setdefault(u, {})[tile] = kronT
-
-        def multiply_scalar(u, tile, first_c):
-            j = UNITS[u][0] // P + tile
+        def multiply_scalar(j, first_c):
             for c in range(first_c, R):
                 nc.scalar.activation(
-                    out=kronT_of[u][:, tile, :, c, :],
+                    out=kronT_of[j][:, :, c, :],
                     in_=pair[:, j, :, :],
                     func=COPY,
                     scale=z2_s[:, j, c : c + 1],
                 )
 
-        def multiply_vector(u, last_c=R):
-            first_tile, tiles = UNITS[u][0] // P, UNITS[u][1] // P
+        def multiply_vector(j, last_c):
             shape = [P, PAIRS, last_c, R * R // PAIRS]
-            for tile in range(tiles):
-                nc.vector.tensor_tensor(
-                    out=kronT_of[u][:, tile, :, 0:last_c, :],
-                    in0=pair[:, first_tile + tile, :, :].unsqueeze(2).to_broadcast(shape),
-                    in1=zT[2][:, first_tile + tile, 0:last_c].unsqueeze(1).unsqueeze(3).to_broadcast(shape),
-                    op=MULT,
-                )
+            nc.vector.tensor_tensor(
+                out=kronT_of[j][:, :, 0:last_c, :],
+                in0=pair[:, j, :, :].unsqueeze(2).to_broadcast(shape),
+                in1=zT[2][:, j, 0:last_c].unsqueeze(1).unsqueeze(3).to_broadcast(shape),
+                op=MULT,
+            )
 
-        def multiply_gpsimd(u, tile):
-            first_tile = UNITS[u][0] // P + tile
-            run = slice(first_tile, first_tile + 1)
+        def multiply_gpsimd(j):
             shape = [P, PAIRS, R, R * R // PAIRS]
             nc.gpsimd.tensor_tensor(
-                out=kronT_of[u][tile][:, 0, :, :, :],
-                in0=pair[:, first_tile, :, :].unsqueeze(2).to_broadcast(shape),
-                in1=z2_s[:, first_tile, :].unsqueeze(1).unsqueeze(3).to_broadcast(shape),
+                out=kronT_of[j][:],
+                in0=pair[:, j, :, :].unsqueeze(2).to_broadcast(shape),
+                in1=z2_s[:, j, :].unsqueeze(1).unsqueeze(3).to_broadcast(shape),
                 op=MULT,
             )
 
@@ -208,8 +197,7 @@ def tile_fast_tucker_taylor_pa_s_kernel(tc, z, G2, out):
             tiles = UNITS[u][1] // P
             turned = psum_turn.tile([P, tiles, PAIRS, P], F32, name="turned")
             for j in range(tiles):
-                kronT = kronT_of[u][j][:, 0] if isinstance(kronT_of[u], dict) else kronT_of[u][:, j]
-                words = kronT.rearrange("s u c x -> s (u c x)").bitcast(F32).rearrange("s (u q) -> s u q", u=PAIRS)
+                words = kronT_of[UNITS[u][0] // P + j][:].rearrange("s u c x -> s (u c x)").bitcast(F32).rearrange("s (u q) -> s u q", u=PAIRS)
                 for half in range(PAIRS):
                     nc.tensor.transpose(
                         out=turned[:, j, half, :], in_=words[:, half, :], identity=ident_f32[:]
@@ -218,7 +206,7 @@ def tile_fast_tucker_taylor_pa_s_kernel(tc, z, G2, out):
 
         def regroup(u):
             tiles = UNITS[u][1] // P
-            pool, name = (keep, "gate") if u == GATE else (work, "grouped")
+            pool, name = (keep, GATES[u]) if u in GATES else (work, "grouped")
             grouped = pool.tile([P, UNITS[u][1] * PACK], BF16, align_bytes=64, name=name)
             nc.scalar.copy(
                 out=grouped[:].bitcast(F32).rearrange("q (j s u) -> q j s u", j=tiles, u=PAIRS),
@@ -229,7 +217,8 @@ def tile_fast_tucker_taylor_pa_s_kernel(tc, z, G2, out):
         def multiply_spread(u):
             first, width = UNITS[u][0] - K_FIRST, UNITS[u][1]
             bank, column = first // BANK, first % BANK
-            grouped = work.tile([P, width * PACK], BF16, align_bytes=64, name="grouped")
+            pool, name = (keep, GATES[u]) if u in GATES else (work, "grouped")
+            grouped = pool.tile([P, width * PACK], BF16, align_bytes=64, name=name)
             nc.vector.tensor_tensor(
                 out=grouped[:].rearrange("q (n t) -> q n t", t=PACK),
                 in0=z0_spread[bank][:, :, column : column + width].rearrange("q t n -> q n t"),
@@ -283,55 +272,61 @@ def tile_fast_tucker_taylor_pa_s_kernel(tc, z, G2, out):
                 in_=gT_ps[:].rearrange("q h u m -> q h m u"),
             )
 
-        samples_unit("n0")
-        samples_unit("n1")
-        samples_unit("n2")
-        gpsimd_tile("g", 0, False)
+        new_kronT(0, keep, "kronT0")
+        new_kronT(1, keep, "kronT1")
+        new_kronT(2, keep, "kronT2")
+        new_kronT(3, keep, "kronT3")
+        new_kronT(4, keep, "kronT4")
+        new_kronT(5, keep, "kronT5")
+        new_kronT(7, keep, "kronT7")
         multiply_w(0)
         multiply_w(1)
-        multiply_gpsimd("g", 0)
-        multiply_scalar("n0", 0, 5)
-        multiply_scalar("n0", 1, 5)
-        multiply_vector("n0", 5)
+        multiply_gpsimd(7)
+        multiply_scalar(0, 5)
+        multiply_scalar(1, 5)
+        multiply_vector(0, 5)
+        multiply_vector(1, 5)
         regroup_g()
         turn("n0")
-        multiply_scalar("n1", 0, 5)
-        multiply_scalar("n1", 1, 5)
-        multiply_vector("n1", 5)
+        multiply_scalar(2, 5)
+        multiply_scalar(3, 5)
+        multiply_vector(2, 5)
+        multiply_vector(3, 5)
         turn_w(0)
-        multiply_scalar("n2", 0, 5)
-        multiply_scalar("n2", 1, 5)
+        multiply_vector(4, 3)
+        multiply_vector(5, 3)
         regroup("n0")
         turn("n1")
-        multiply_vector("n2", 5)
+        multiply_scalar(4, 3)
         regroup("n1")
-        turn("n2")
+        multiply_scalar(5, 3)
         multiply_spread("k0")
-        turn_w(1)
-        regroup("n2")
         quantise_g()
         quantise("n0")
         product("n0")
-        store("n0", "scalar")
         quantise("n1")
         product("n1")
-        gpsimd_tile("g", 1, True)
-        multiply_gpsimd("g", 1)
+        turn("n2")
+        turn_w(1)
+        store("n0", "scalar")
+        new_kronT(6, keep, "gate")
+        multiply_gpsimd(6)
         store("n1", "scalar")
         multiply_spread("k1")
         quantise("k0")
         product("k0")
-        turn("g")
+        regroup("n2")
         store("k0", "scalar")
-        quantise("n2")
-        product("n2")
-        regroup("g")
-        store("n2", "scalar")
+        turn("g")
         quantise("k1")
         product("k1")
+        regroup("g")
         multiply_spread("k2")
         store("k1", "scalar")
+        quantise("n2")
+        product("n2")
         multiply_spread("k3")
+        store("n2", "scalar")
         quantise("g")
         product("g")
         store("g", "scalar")

@@ -40,6 +40,8 @@ UNITS = {
 }
 PAIR_RUNS = (slice(0, 2), slice(2, 8))
 GATES = {"n1": "gate"}
+W_CALLS = ((8, 10), (10, 16))
+W_TILES = ((8, 10), (10, 12), (12, 16))
 LAST = "k4"
 
 FLOPS = 2 * M * K * N
@@ -62,15 +64,15 @@ def tile_fast_tucker_taylor_pa_s_kernel(tc, z, G2, out):
         g_rows = keep.tile([P, M_TILES, K], BF16)
         nc.sync.dma_start(out=g_rows[:], in_=G2.rearrange("(h m) k -> m h k", m=P))
         z0_spread = []
-        for bank in range(K_TILES * P // BANK):
-            spread = keep.tile([P, PACK, BANK], BF16, name="z0_spread%d" % bank)
-            columns = slice(K_FIRST + bank * BANK, K_FIRST + (bank + 1) * BANK)
+        for first, last in W_TILES:
+            width = (last - first) * P
+            spread = keep.tile([P, PACK, width], BF16, name="z0_spread%d" % first)
             for half in range(2):
                 nc.sync.dma_start(
                     out=spread[half::2, :, :],
-                    in_=z[0, PACK * half : PACK * (half + 1), columns]
+                    in_=z[0, PACK * half : PACK * (half + 1), first * P : last * P]
                     .unsqueeze(0)
-                    .to_broadcast([P // 2, PACK, BANK]),
+                    .to_broadcast([P // 2, PACK, width]),
                 )
             z0_spread.append(spread)
 
@@ -139,26 +141,28 @@ def tile_fast_tucker_taylor_pa_s_kernel(tc, z, G2, out):
         acc_of = {}
 
         wT_of = {}
-        bank_tiles = BANK // P
 
-        def multiply_w(bank):
-            run = slice(bank * bank_tiles, (bank + 1) * bank_tiles)
-            shape = [P, bank_tiles, R, 2 * R]
-            wT = keep.tile(shape, F32, name="wT%d" % bank)
+        def multiply_w(call):
+            first, last = W_CALLS[call]
+            run = slice(first - S_TILES, last - S_TILES)
+            shape = [P, last - first, R, 2 * R]
+            wT = keep.tile(shape, F32, name="wT%d" % call)
             nc.gpsimd.tensor_tensor(
                 out=wT[:],
                 in0=z2_k[:, run, :].unsqueeze(3).to_broadcast(shape),
                 in1=z1_k[:, run, :, :].rearrange("s j b d -> s j (b d)").unsqueeze(2).to_broadcast(shape),
                 op=MULT,
             )
-            wT_of[bank] = wT
+            for j in range(first, last):
+                wT_of[j] = wT[:, j - first, :, :].rearrange("s c x -> s (c x)")
 
         def turn_w(bank):
-            w_ps = psum_w.tile([P, BANK], F32, name="w_ps")
+            bank_tiles = W_TILES[bank][1] - W_TILES[bank][0]
+            w_ps = psum_w.tile([P, bank_tiles * P], F32, name="w_ps")
             for j in range(bank_tiles):
                 nc.tensor.transpose(
                     out=w_ps[:, j * P : (j + 1) * P],
-                    in_=wT_of[bank][:, j, :, :].rearrange("s c x -> s (c x)"),
+                    in_=wT_of[W_TILES[bank][0] + j],
                     identity=ident_f32[:],
                 )
             w_of_bank[bank] = w_ps
@@ -166,8 +170,8 @@ def tile_fast_tucker_taylor_pa_s_kernel(tc, z, G2, out):
         def new_kronT(j, pool, name):
             kronT_of[j] = pool.tile([P, PAIRS, R, R * R // PAIRS], BF16, align_bytes=64, name=name)
 
-        def multiply_scalar(j, first_c):
-            for c in range(first_c, R):
+        def multiply_scalar(j, first_c, last_c=R):
+            for c in range(first_c, last_c):
                 nc.scalar.activation(
                     out=kronT_of[j][:, :, c, :],
                     in_=pair[:, j, :, :],
@@ -184,12 +188,12 @@ def tile_fast_tucker_taylor_pa_s_kernel(tc, z, G2, out):
                 op=MULT,
             )
 
-        def multiply_gpsimd(j):
-            shape = [P, PAIRS, R, R * R // PAIRS]
+        def multiply_gpsimd(j, last_c=R):
+            shape = [P, PAIRS, last_c, R * R // PAIRS]
             nc.gpsimd.tensor_tensor(
-                out=kronT_of[j][:],
+                out=kronT_of[j][:, :, 0:last_c, :],
                 in0=pair[:, j, :, :].unsqueeze(2).to_broadcast(shape),
-                in1=z2_s[:, j, :].unsqueeze(1).unsqueeze(3).to_broadcast(shape),
+                in1=z2_s[:, j, 0:last_c].unsqueeze(1).unsqueeze(3).to_broadcast(shape),
                 op=MULT,
             )
 
@@ -215,8 +219,9 @@ def tile_fast_tucker_taylor_pa_s_kernel(tc, z, G2, out):
             grouped_of[u] = grouped
 
         def multiply_spread(u):
-            first, width = UNITS[u][0] - K_FIRST, UNITS[u][1]
-            bank, column = first // BANK, first % BANK
+            width = UNITS[u][1]
+            bank = [i for i, (a, b) in enumerate(W_TILES) if a * P <= UNITS[u][0] < b * P][0]
+            column = UNITS[u][0] - W_TILES[bank][0] * P
             pool, name = (keep, GATES[u]) if u in GATES else (work, "grouped")
             grouped = pool.tile([P, width * PACK], BF16, align_bytes=64, name=name)
             nc.vector.tensor_tensor(
@@ -281,33 +286,35 @@ def tile_fast_tucker_taylor_pa_s_kernel(tc, z, G2, out):
         new_kronT(7, keep, "kronT7")
         multiply_w(0)
         multiply_w(1)
-        multiply_gpsimd(7)
+        multiply_gpsimd(7, 4)
         multiply_scalar(0, 5)
         multiply_scalar(1, 5)
         multiply_vector(0, 5)
         multiply_vector(1, 5)
         regroup_g()
+        turn_w(0)
         turn("n0")
         multiply_scalar(2, 5)
         multiply_scalar(3, 5)
         multiply_vector(2, 5)
         multiply_vector(3, 5)
-        turn_w(0)
-        multiply_vector(4, 3)
-        multiply_vector(5, 3)
         regroup("n0")
         turn("n1")
+        turn_w(1)
+        multiply_vector(4, 3)
+        multiply_vector(5, 3)
         multiply_scalar(4, 3)
         regroup("n1")
-        multiply_scalar(5, 3)
         multiply_spread("k0")
+        turn_w(2)
+        multiply_scalar(5, 3)
         quantise_g()
         quantise("n0")
         product("n0")
         quantise("n1")
         product("n1")
         turn("n2")
-        turn_w(1)
+        multiply_scalar(7, 4)
         store("n0", "scalar")
         new_kronT(6, keep, "gate")
         multiply_gpsimd(6)

@@ -39,7 +39,8 @@ UNITS = {
     "k4": (1920, 128),
 }
 PAIR_RUNS = (slice(0, 2), slice(2, 8))
-GATES = {"n1": "gate"}
+GATES = {"k0": "gate"}
+LOADS = ((8, 12), (12, 16))
 W_CALLS = ((8, 10), (10, 16))
 W_TILES = ((8, 10), (10, 12), (12, 16))
 LAST = "k4"
@@ -63,8 +64,8 @@ def tile_fast_tucker_taylor_pa_s_kernel(tc, z, G2, out):
             nc.sync.dma_start(out=z_rows[:, i, :], in_=z[i].rearrange("a (j s) -> (a j) s", s=P))
         g_rows = keep.tile([P, M_TILES, K], BF16)
         nc.sync.dma_start(out=g_rows[:], in_=G2.rearrange("(h m) k -> m h k", m=P))
-        z0_spread = []
-        for first, last in W_TILES:
+        z0_spread = {}
+        for first, last in LOADS:
             width = (last - first) * P
             spread = keep.tile([P, PACK, width], BF16, name="z0_spread%d" % first)
             for half in range(2):
@@ -74,7 +75,8 @@ def tile_fast_tucker_taylor_pa_s_kernel(tc, z, G2, out):
                     .unsqueeze(0)
                     .to_broadcast([P // 2, PACK, width]),
                 )
-            z0_spread.append(spread)
+            for j in range(first, last):
+                z0_spread[j] = (spread, first)
 
         ident_bf16 = keep.tile([P, P], BF16)
         make_identity(nc, ident_bf16[:])
@@ -222,11 +224,13 @@ def tile_fast_tucker_taylor_pa_s_kernel(tc, z, G2, out):
             width = UNITS[u][1]
             bank = [i for i, (a, b) in enumerate(W_TILES) if a * P <= UNITS[u][0] < b * P][0]
             column = UNITS[u][0] - W_TILES[bank][0] * P
+            spread, spread_first = z0_spread[UNITS[u][0] // P]
+            from_column = UNITS[u][0] - spread_first * P
             pool, name = (keep, GATES[u]) if u in GATES else (work, "grouped")
             grouped = pool.tile([P, width * PACK], BF16, align_bytes=64, name=name)
             nc.vector.tensor_tensor(
                 out=grouped[:].rearrange("q (n t) -> q n t", t=PACK),
-                in0=z0_spread[bank][:, :, column : column + width].rearrange("q t n -> q n t"),
+                in0=spread[:, :, from_column : from_column + width].rearrange("q t n -> q n t"),
                 in1=w_of_bank[bank][:, column : column + width].unsqueeze(2).to_broadcast([P, width, PACK]),
                 op=MULT,
             )
@@ -313,6 +317,8 @@ def tile_fast_tucker_taylor_pa_s_kernel(tc, z, G2, out):
         product("n0")
         quantise("n1")
         product("n1")
+        quantise("k0")
+        product("k0")
         turn("n2")
         multiply_scalar(7, 4)
         store("n0", "scalar")
@@ -320,10 +326,9 @@ def tile_fast_tucker_taylor_pa_s_kernel(tc, z, G2, out):
         multiply_gpsimd(6)
         store("n1", "scalar")
         multiply_spread("k1")
-        quantise("k0")
-        product("k0")
-        regroup("n2")
+        multiply_spread("k3")
         store("k0", "scalar")
+        regroup("n2")
         turn("g")
         quantise("k1")
         product("k1")
@@ -332,15 +337,14 @@ def tile_fast_tucker_taylor_pa_s_kernel(tc, z, G2, out):
         store("k1", "scalar")
         quantise("n2")
         product("n2")
-        multiply_spread("k3")
+        quantise("k2")
+        product("k2")
         store("n2", "scalar")
         quantise("g")
         product("g")
-        store("g", "scalar")
-        quantise("k2")
-        product("k2")
         store("k2", "scalar")
         multiply_spread("k4")
+        store("g", "scalar")
         quantise("k3")
         product("k3")
         store("k3", "scalar")

@@ -90,13 +90,31 @@ def tile_fast_tucker_taylor_pa_s_kernel(tc, z, G2, out):
                 in_=ident_bf16[:].rearrange("p (d u e j) -> p u j d e", d=2, u=PAIRS, e=2)[:, u, :, :, :],
             )
 
+        twice = keep.tile([P, S_TILES, PAIRS, R], BF16)
+        nc.vector.tensor_copy(
+            out=twice[:],
+            in_=ident_bf16[:]
+            .rearrange("p (c j) -> p j c", c=R)[:, 0:S_TILES, :]
+            .unsqueeze(2)
+            .to_broadcast([P, S_TILES, PAIRS, R]),
+        )
+
         zT = {}
         for i in FACTOR_ORDER:
-            pool = psum_once if i == 2 else psum_acc
-            zT_ps = pool.tile([P, P], BF16, name="zT2" if i == 2 else "acc")
+            pool, name = (psum_w, "w_ps") if i == 2 else (psum_acc, "acc")
+            zT_ps = pool.tile([P, P], BF16, name=name)
             order = ident_order[:].rearrange("p j u d e -> p (j u d e)") if i == 0 else ident_bf16[:]
             nc.tensor.transpose(out=zT_ps[:], in_=z_rows[:, i, :], identity=order)
             zT[i] = zT_ps[:] if i == 0 else zT_ps[:].rearrange("s (a j) -> s j a", j=N_TILES)
+
+        z2_twice = psum_once.tile([P, S_TILES * PAIRS, R], F32)
+        nc.tensor.matmul(
+            out=z2_twice[:].rearrange("s h c -> s (h c)"),
+            lhsT=z_rows[:, 2, :],
+            rhs=twice[:].rearrange("p j u c -> p (j u c)"),
+            start=True,
+            stop=True,
+        )
 
         z1_s = keep.tile([P, S_TILES, PAIRS, R], F32)
         nc.vector.tensor_copy(
@@ -112,7 +130,7 @@ def tile_fast_tucker_taylor_pa_s_kernel(tc, z, G2, out):
                 in1=z1_s[:].rearrange("s j u b -> s (j u) b")[:, halves, :].unsqueeze(3).to_broadcast(shape),
                 op=MULT,
             )
-        pair = pair[:].rearrange("s (j u) b x -> s j u (b x)", u=PAIRS)
+        pair = pair[:].rearrange("s h b x -> s h (b x)")
 
         z1_k = keep.tile([P, K_TILES, R, 2], F32)
         nc.scalar.copy(
@@ -169,24 +187,34 @@ def tile_fast_tucker_taylor_pa_s_kernel(tc, z, G2, out):
                 )
             w_of_bank[bank] = w_ps
 
+        def new_unit(u):
+            tiles = UNITS[u][1] // P
+            kronT = keep.tile([P, tiles, PAIRS, R, R * R // PAIRS], BF16, name="kronT_" + u)
+            kronT_of[u] = kronT
+            for tile in range(tiles):
+                kronT_of[UNITS[u][0] // P + tile] = kronT[:, tile, :, :, :]
+
         def new_kronT(j, pool, name):
-            kronT_of[j] = pool.tile([P, PAIRS, R, R * R // PAIRS], BF16, align_bytes=64, name=name)
+            kronT = pool.tile([P, PAIRS, R, R * R // PAIRS], BF16, align_bytes=64, name=name)
+            kronT_of[j] = kronT[:]
 
         def multiply_scalar(j, first_c, last_c=R):
             for c in range(first_c, last_c):
                 nc.scalar.activation(
                     out=kronT_of[j][:, :, c, :],
-                    in_=pair[:, j, :, :],
+                    in_=pair[:, j * PAIRS : (j + 1) * PAIRS, :],
                     func=COPY,
                     scale=z2_s[:, j, c : c + 1],
                 )
 
-        def multiply_vector(j, last_c):
-            shape = [P, PAIRS, last_c, R * R // PAIRS]
+        def multiply_vector(u, last_c):
+            first_tile, tiles = UNITS[u][0] // P, UNITS[u][1] // P
+            halves = slice(first_tile * PAIRS, (first_tile + tiles) * PAIRS)
+            shape = [P, tiles * PAIRS, last_c, R * R // PAIRS]
             nc.vector.tensor_tensor(
-                out=kronT_of[j][:, :, 0:last_c, :],
-                in0=pair[:, j, :, :].unsqueeze(2).to_broadcast(shape),
-                in1=zT[2][:, j, 0:last_c].unsqueeze(1).unsqueeze(3).to_broadcast(shape),
+                out=kronT_of[u][:].rearrange("s j u c x -> s (j u) c x")[:, :, 0:last_c, :],
+                in0=pair[:, halves, :].unsqueeze(2).to_broadcast(shape),
+                in1=z2_twice[:, halves, 0:last_c].unsqueeze(3).to_broadcast(shape),
                 op=MULT,
             )
 
@@ -194,7 +222,7 @@ def tile_fast_tucker_taylor_pa_s_kernel(tc, z, G2, out):
             shape = [P, PAIRS, last_c, R * R // PAIRS]
             nc.gpsimd.tensor_tensor(
                 out=kronT_of[j][:, :, 0:last_c, :],
-                in0=pair[:, j, :, :].unsqueeze(2).to_broadcast(shape),
+                in0=pair[:, j * PAIRS : (j + 1) * PAIRS, :].unsqueeze(2).to_broadcast(shape),
                 in1=z2_s[:, j, 0:last_c].unsqueeze(1).unsqueeze(3).to_broadcast(shape),
                 op=MULT,
             )
@@ -203,7 +231,7 @@ def tile_fast_tucker_taylor_pa_s_kernel(tc, z, G2, out):
             tiles = UNITS[u][1] // P
             turned = psum_turn.tile([P, tiles, PAIRS, P], F32, name="turned")
             for j in range(tiles):
-                words = kronT_of[UNITS[u][0] // P + j][:].rearrange("s u c x -> s (u c x)").bitcast(F32).rearrange("s (u q) -> s u q", u=PAIRS)
+                words = kronT_of[UNITS[u][0] // P + j].rearrange("s u c x -> s (u c x)").bitcast(F32).rearrange("s (u q) -> s u q", u=PAIRS)
                 for half in range(PAIRS):
                     nc.tensor.transpose(
                         out=turned[:, j, half, :], in_=words[:, half, :], identity=ident_f32[:]
@@ -281,68 +309,62 @@ def tile_fast_tucker_taylor_pa_s_kernel(tc, z, G2, out):
                 in_=gT_ps[:].rearrange("q h u m -> q h m u"),
             )
 
-        new_kronT(0, keep, "kronT0")
-        new_kronT(1, keep, "kronT1")
-        new_kronT(2, keep, "kronT2")
-        new_kronT(3, keep, "kronT3")
-        new_kronT(4, keep, "kronT4")
-        new_kronT(5, keep, "kronT5")
+        new_unit("n0")
+        new_unit("n1")
+        new_unit("n2")
         new_kronT(7, keep, "kronT7")
         multiply_w(0)
         multiply_w(1)
         multiply_gpsimd(7, 4)
-        multiply_scalar(0, 5)
-        multiply_scalar(1, 5)
-        multiply_vector(0, 5)
-        multiply_vector(1, 5)
+        multiply_scalar(0, 6)
+        multiply_scalar(1, 6)
+        multiply_vector("n0", 6)
         regroup_g()
         turn_w(0)
         turn("n0")
-        multiply_scalar(2, 5)
-        multiply_scalar(3, 5)
-        multiply_vector(2, 5)
-        multiply_vector(3, 5)
+        multiply_scalar(2, 6)
+        multiply_scalar(3, 6)
+        multiply_vector("n1", 6)
         regroup("n0")
         turn("n1")
         turn_w(1)
-        multiply_vector(4, 3)
-        multiply_vector(5, 3)
-        multiply_scalar(4, 3)
+        multiply_vector("n2", 4)
         regroup("n1")
         multiply_spread("k0")
         turn_w(2)
-        multiply_scalar(5, 3)
+        multiply_scalar(4, 4)
+        multiply_scalar(5, 4)
         quantise_g()
         quantise("n0")
         product("n0")
         quantise("n1")
         product("n1")
         quantise("k0")
-        product("k0")
-        turn("n2")
         multiply_scalar(7, 4)
+        turn("n2")
         store("n0", "scalar")
         new_kronT(6, keep, "gate")
         multiply_gpsimd(6)
         store("n1", "scalar")
         multiply_spread("k1")
-        multiply_spread("k3")
-        store("k0", "scalar")
+        product("k0")
         regroup("n2")
+        multiply_spread("k2")
+        store("k0", "scalar")
         turn("g")
+        regroup("g")
         quantise("k1")
         product("k1")
-        regroup("g")
-        multiply_spread("k2")
-        store("k1", "scalar")
         quantise("n2")
         product("n2")
+        store("k1", "scalar")
         quantise("k2")
         product("k2")
         store("n2", "scalar")
         quantise("g")
         product("g")
         store("k2", "scalar")
+        multiply_spread("k3")
         multiply_spread("k4")
         store("g", "scalar")
         quantise("k3")

from contextlib import ExitStack

import concourse.mybir as mybir
from concourse.masks import make_identity

F32 = mybir.dt.float32
BF16 = mybir.dt.bfloat16
U32 = mybir.dt.uint32
U8 = mybir.dt.uint8
FP8X4 = mybir.dt.float8_e4m3fn_x4
MULT = mybir.AluOpType.mult
COPY = mybir.ActivationFunctionType.Copy

P = 128
ORD = 3
FACTOR_ORDER = (1, 0, 2)
R = 8
K = R**ORD
PACK = 4
PAIRS = 2
N = 2048
M = 256
N_TILES = N // P
M_TILES = M // P
BANK = 512

S_TILES = 8
K_TILES = N_TILES - S_TILES
K_FIRST = S_TILES * P
UNITS = {
    "n0": (0, 256),
    "n1": (256, 256),
    "n2": (512, 256),
    "g": (768, 256),
    "k0": (1024, 256),
    "k1": (1280, 256),
    "k2": (1536, 256),
    "k3": (1792, 128),
    "k4": (1920, 128),
}
PAIR_RUNS = (slice(0, 2), slice(2, 8))
GATES = {"k0": "gate"}
LOADS = ((8, 12), (12, 16))
W_CALLS = ((8, 10), (10, 16))
W_TILES = ((8, 10), (10, 12), (12, 16))
LAST = "k4"

FLOPS = 2 * M * K * N


def tile_fast_tucker_taylor_pa_s_kernel(tc, z, G2, out):
    nc = tc.nc
    with ExitStack() as ctx:
        keep = ctx.enter_context(tc.tile_pool(name="keep", bufs=1))
        work = ctx.enter_context(tc.tile_pool(name="work", bufs=5))
        psum_once = ctx.enter_context(tc.psum_pool(name="psum_once", bufs=1))
        psum_turn = ctx.enter_context(tc.psum_pool(name="psum_turn", bufs=2))
        psum_w = ctx.enter_context(tc.psum_pool(name="psum_w", bufs=2))
        psum_acc = ctx.enter_context(tc.psum_pool(name="psum_acc", bufs=3))
        ctx.enter_context(tc.manual_schedule())

        z_rows = keep.tile([P, ORD, P], BF16)
        for i in FACTOR_ORDER:
            nc.sync.dma_start(out=z_rows[:, i, :], in_=z[i].rearrange("a (j s) -> (a j) s", s=P))
        g_rows = keep.tile([P, M_TILES, K], BF16)
        nc.sync.dma_start(out=g_rows[:], in_=G2.rearrange("(h m) k -> m h k", m=P))
        z0_spread = {}
        for first, last in LOADS:
            width = (last - first) * P
            spread = keep.tile([P, PACK, width], BF16, name="z0_spread%d" % first)
            for half in range(2):
                nc.sync.dma_start(
                    out=spread[half::2, :, :],
                    in_=z[0, PACK * half : PACK * (half + 1), first * P : last * P]
                    .unsqueeze(0)
                    .to_broadcast([P // 2, PACK, width]),
                )
            for j in range(first, last):
                z0_spread[j] = (spread, first)

        ident_bf16 = keep.tile([P, P], BF16)
        make_identity(nc, ident_bf16[:])
        ident_f32 = keep.tile([P, P], F32)
        make_identity(nc, ident_f32[:])

        ident_order = keep.tile([P, N_TILES, PAIRS, 2, 2], BF16)
        for u in range(PAIRS):
            nc.vector.tensor_copy(
                out=ident_order[:, :, u, :, :],
                in_=ident_bf16[:].rearrange("p (d u e j) -> p u j d e", d=2, u=PAIRS, e=2)[:, u, :, :, :],
            )

        twice = keep.tile([P, S_TILES, PAIRS, R], BF16)
        nc.vector.tensor_copy(
            out=twice[:],
            in_=ident_bf16[:]
            .rearrange("p (c j) -> p j c", c=R)[:, 0:S_TILES, :]
            .unsqueeze(2)
            .to_broadcast([P, S_TILES, PAIRS, R]),
        )

        zT = {}
        for i in FACTOR_ORDER:
            pool, name = (psum_w, "w_ps") if i == 2 else (psum_acc, "acc")
            zT_ps = pool.tile([P, P], BF16, name=name)
            order = ident_order[:].rearrange("p j u d e -> p (j u d e)") if i == 0 else ident_bf16[:]
            nc.tensor.transpose(out=zT_ps[:], in_=z_rows[:, i, :], identity=order)
            zT[i] = zT_ps[:] if i == 0 else zT_ps[:].rearrange("s (a j) -> s j a", j=N_TILES)

        z2_twice = psum_once.tile([P, S_TILES * PAIRS, R], F32)
        nc.tensor.matmul(
            out=z2_twice[:].rearrange("s h c -> s (h c)"),
            lhsT=z_rows[:, 2, :],
            rhs=twice[:].rearrange("p j u c -> p (j u c)"),
            start=True,
            stop=True,
        )

        z1_s = keep.tile([P, S_TILES, PAIRS, R], F32)
        nc.vector.tensor_copy(
            out=z1_s[:], in_=zT[1][:, 0:S_TILES, :].unsqueeze(2).to_broadcast([P, S_TILES, PAIRS, R])
        )
        pair = keep.tile([P, S_TILES * PAIRS, R, 4], F32)
        for run in PAIR_RUNS:
            halves = slice(run.start * PAIRS, run.stop * PAIRS)
            shape = [P, halves.stop - halves.start, R, 4]
            nc.vector.tensor_tensor(
                out=pair[:, halves, :, :],
                in0=zT[0].rearrange("s (h x) -> s h x", x=4)[:, halves, :].unsqueeze(2).to_broadcast(shape),
                in1=z1_s[:].rearrange("s j u b -> s (j u) b")[:, halves, :].unsqueeze(3).to_broadcast(shape),
                op=MULT,
            )
        pair = pair[:].rearrange("s h b x -> s h (b x)")

        z1_k = keep.tile([P, K_TILES, R, 2], F32)
        nc.scalar.copy(
            out=z1_k[:],
            in_=zT[1][:, S_TILES:N_TILES, :].unsqueeze(3).to_broadcast([P, K_TILES, R, 2]),
        )
        z2_k = keep.tile([P, K_TILES, R], F32)
        nc.scalar.copy(out=z2_k[:], in_=zT[2][:, S_TILES:N_TILES, :])
        z2_s = keep.tile([P, S_TILES, R], F32)
        nc.scalar.copy(out=z2_s[:], in_=zT[2][:, 0:S_TILES, :])
        g_words = g_rows[:].bitcast(F32).rearrange("m h (q u) -> m h q u", u=PAIRS)
        gT_ps = psum_acc.tile([P, M_TILES, PAIRS, P], F32, name="acc")
        for h in range(M_TILES):
            for u in range(PAIRS):
                nc.tensor.transpose(
                    out=gT_ps[:, h, u, :], in_=g_words[:, h, :, u], identity=ident_f32[:]
                )
        g_grouped = keep.tile([P, M * PACK], BF16, align_bytes=64)
        g_codes = keep.tile([P, M], U32, align_bytes=64)
        g_scales = keep.tile([P, M], U8, align_bytes=64)

        out_by_half = out.rearrange("(h m) n -> m h n", m=P)
        w_of_bank = {}
        kronT_of = {}
        turned_of = {}
        grouped_of = {}
        codes_of = {}
        acc_of = {}

        wT_of = {}

        def multiply_w(call):
            first, last = W_CALLS[call]
            run = slice(first - S_TILES, last - S_TILES)
            shape = [P, last - first, R, 2 * R]
            wT = keep.tile(shape, F32, name="wT%d" % call)
            nc.gpsimd.tensor_tensor(
                out=wT[:],
                in0=z2_k[:, run, :].unsqueeze(3).to_broadcast(shape),
                in1=z1_k[:, run, :, :].rearrange("s j b d -> s j (b d)").unsqueeze(2).to_broadcast(shape),
                op=MULT,
            )
            for j in range(first, last):
                wT_of[j] = wT[:, j - first, :, :].rearrange("s c x -> s (c x)")

        def turn_w(bank):
            bank_tiles = W_TILES[bank][1] - W_TILES[bank][0]
            w_ps = psum_w.tile([P, bank_tiles * P], F32, name="w_ps")
            for j in range(bank_tiles):
                nc.tensor.transpose(
                    out=w_ps[:, j * P : (j + 1) * P],
                    in_=wT_of[W_TILES[bank][0] + j],
                    identity=ident_f32[:],
                )
            w_of_bank[bank] = w_ps

        def new_unit(u):
            tiles = UNITS[u][1] // P
            kronT = keep.tile([P, tiles, PAIRS, R, R * R // PAIRS], BF16, name="kronT_" + u)
            kronT_of[u] = kronT
            for tile in range(tiles):
                kronT_of[UNITS[u][0] // P + tile] = kronT[:, tile, :, :, :]

        def new_kronT(j, pool, name):
            kronT = pool.tile([P, PAIRS, R, R * R // PAIRS], BF16, align_bytes=64, name=name)
            kronT_of[j] = kronT[:]

        def multiply_scalar(j, first_c, last_c=R):
            for c in range(first_c, last_c):
                nc.scalar.activation(
                    out=kronT_of[j][:, :, c, :],
                    in_=pair[:, j * PAIRS : (j + 1) * PAIRS, :],
                    func=COPY,
                    scale=z2_s[:, j, c : c + 1],
                )

        def multiply_vector(u, last_c):
            first_tile, tiles = UNITS[u][0] // P, UNITS[u][1] // P
            halves = slice(first_tile * PAIRS, (first_tile + tiles) * PAIRS)
            shape = [P, tiles * PAIRS, last_c, R * R // PAIRS]
            nc.vector.tensor_tensor(
                out=kronT_of[u][:].rearrange("s j u c x -> s (j u) c x")[:, :, 0:last_c, :],
                in0=pair[:, halves, :].unsqueeze(2).to_broadcast(shape),
                in1=z2_twice[:, halves, 0:last_c].unsqueeze(3).to_broadcast(shape),
                op=MULT,
            )

        def multiply_gpsimd(j, last_c=R):
            shape = [P, PAIRS, last_c, R * R // PAIRS]
            nc.gpsimd.tensor_tensor(
                out=kronT_of[j][:, :, 0:last_c, :],
                in0=pair[:, j * PAIRS : (j + 1) * PAIRS, :].unsqueeze(2).to_broadcast(shape),
                in1=z2_s[:, j, 0:last_c].unsqueeze(1).unsqueeze(3).to_broadcast(shape),
                op=MULT,
            )

        def turn(u):
            tiles = UNITS[u][1] // P
            turned = psum_turn.tile([P, tiles, PAIRS, P], F32, name="turned")
            for j in range(tiles):
                words = kronT_of[UNITS[u][0] // P + j].rearrange("s u c x -> s (u c x)").bitcast(F32).rearrange("s (u q) -> s u q", u=PAIRS)
                for half in range(PAIRS):
                    nc.tensor.transpose(
                        out=turned[:, j, half, :], in_=words[:, half, :], identity=ident_f32[:]
                    )
            turned_of[u] = turned

        def regroup(u):
            tiles = UNITS[u][1] // P
            pool, name = (keep, GATES[u]) if u in GATES else (work, "grouped")
            grouped = pool.tile([P, UNITS[u][1] * PACK], BF16, align_bytes=64, name=name)
            nc.scalar.copy(
                out=grouped[:].bitcast(F32).rearrange("q (j s u) -> q j s u", j=tiles, u=PAIRS),
                in_=turned_of[u][:].rearrange("q j u s -> q j s u"),
            )
            grouped_of[u] = grouped

        def multiply_spread(u):
            width = UNITS[u][1]
            bank = [i for i, (a, b) in enumerate(W_TILES) if a * P <= UNITS[u][0] < b * P][0]
            column = UNITS[u][0] - W_TILES[bank][0] * P
            spread, spread_first = z0_spread[UNITS[u][0] // P]
            from_column = UNITS[u][0] - spread_first * P
            pool, name = (keep, GATES[u]) if u in GATES else (work, "grouped")
            grouped = pool.tile([P, width * PACK], BF16, align_bytes=64, name=name)
            nc.vector.tensor_tensor(
                out=grouped[:].rearrange("q (n t) -> q n t", t=PACK),
                in0=spread[:, :, from_column : from_column + width].rearrange("q t n -> q n t"),
                in1=w_of_bank[bank][:, column : column + width].unsqueeze(2).to_broadcast([P, width, PACK]),
                op=MULT,
            )
            grouped_of[u] = grouped

        def quantise(u):
            k_codes = work.tile([P, UNITS[u][1]], U32, align_bytes=64, name="k_codes")
            k_scales = work.tile([P, UNITS[u][1]], U8, align_bytes=64, name="k_scales")
            nc.vector.quantize_mx(
                out=k_codes[:].bitcast(FP8X4), scales=k_scales[:], in_=grouped_of[u][:]
            )
            codes_of[u] = (k_codes, k_scales)

        def product(u):
            k_codes, k_scales = codes_of[u]
            pool, name = (psum_w, "w_ps") if u == LAST else (psum_acc, "acc")
            acc = pool.tile([P, M_TILES, UNITS[u][1]], F32, name=name)
            for h in range(M_TILES):
                rows = slice(h * P, (h + 1) * P)
                nc.tensor.matmul_mx(
                    out=acc[:, h, :],
                    lhsT=g_codes[:, rows].bitcast(FP8X4),
                    lhsT_scale=g_scales[:, rows],
                    rhs=k_codes[:].bitcast(FP8X4),
                    rhs_scale=k_scales[:],
                    start=True,
                    stop=True,
                )
            acc_of[u] = acc

        def store(u, engine):
            first, width = UNITS[u]
            result = keep.tile([P, M_TILES, width], F32, name="result_" + u)
            if engine == "vector":
                nc.vector.tensor_copy(out=result[:], in_=acc_of[u][:])
            else:
                nc.scalar.copy(out=result[:], in_=acc_of[u][:])
            nc.sync.dma_start(out=out_by_half[:, :, first : first + width], in_=result[:])

        def quantise_g():
            nc.vector.quantize_mx(
                out=g_codes[:].bitcast(FP8X4), scales=g_scales[:], in_=g_grouped[:]
            )

        def regroup_g():
            nc.scalar.copy(
                out=g_grouped[:].bitcast(F32).rearrange("q (h m u) -> q h m u", h=M_TILES, u=PAIRS),
                in_=gT_ps[:].rearrange("q h u m -> q h m u"),
            )

        new_unit("n0")
        new_unit("n1")
        new_unit("n2")
        new_kronT(7, keep, "kronT7")
        multiply_w(0)
        multiply_w(1)
        multiply_gpsimd(7, 4)
        multiply_scalar(0, 6)
        multiply_scalar(1, 6)
        multiply_vector("n0", 6)
        regroup_g()
        turn_w(0)
        turn("n0")
        multiply_scalar(2, 6)
        multiply_scalar(3, 6)
        multiply_vector("n1", 6)
        regroup("n0")
        turn("n1")
        turn_w(1)
        multiply_vector("n2", 4)
        regroup("n1")
        multiply_spread("k0")
        turn_w(2)
        multiply_scalar(4, 4)
        multiply_scalar(5, 4)
        quantise_g()
        quantise("n0")
        product("n0")
        quantise("n1")
        product("n1")
        quantise("k0")
        multiply_scalar(7, 4)
        turn("n2")
        store("n0", "scalar")
        new_kronT(6, keep, "gate")
        multiply_gpsimd(6)
        store("n1", "scalar")
        multiply_spread("k1")
        product("k0")
        regroup("n2")
        multiply_spread("k2")
        store("k0", "scalar")
        turn("g")
        regroup("g")
        quantise("k1")
        product("k1")
        quantise("n2")
        product("n2")
        store("k1", "scalar")
        quantise("k2")
        product("k2")
        store("n2", "scalar")
        quantise("g")
        product("g")
        store("k2", "scalar")
        multiply_spread("k3")
        multiply_spread("k4")
        store("g", "scalar")
        quantise("k3")
        product("k3")
        store("k3", "scalar")
        quantise("k4")
        product("k4")
        store("k4", "vector")
